import numpy as np
import ml_dtypes


def mxq(x, axis, fmt="e4m3"):
    dtype, down = {"e4m3": (ml_dtypes.float8_e4m3fn, 7), "e5m2": (ml_dtypes.float8_e5m2, 14)}[fmt]
    v = np.moveaxis(np.asarray(x, np.float32).astype(ml_dtypes.bfloat16).astype(np.float64), axis, -1)
    blocks = v.reshape(v.shape[:-1] + (-1, 32))
    amax = np.abs(blocks).max(-1, keepdims=True)
    byte = np.maximum(np.where(amax > 0, np.frexp(amax)[1] - 1 + 127, 0) - down, 1)
    scale = np.exp2(byte - 127.0)
    codes = (blocks / scale).astype(np.float32).astype(dtype).astype(np.float64)
    return np.moveaxis((codes * scale).reshape(v.shape), -1, axis)


WIDE = False


def mx_kscale(k):
    if not WIDE:
        return np.ones(k)
    levels = np.array([10, -10, 5, -5, 0])
    a = np.random.permutation(np.resize(levels, k // 512 * 4)).reshape(k // 512, 4)
    idx = np.arange(k)
    return np.exp2(a[idx // 512, idx % 128 // 32])


BF16 = ml_dtypes.bfloat16


def bf(x):
    return np.asarray(x, np.float32).astype(BF16)


def f64(x):
    return np.asarray(x).astype(np.float64)


B, C, NB, BW, T, EMB = 4, 2, 2, 256, 1024, 512
F = NB * BW
FEAT = C * BW * 2
EPS = 1e-5


def setup_inputs():
    s = mx_kscale(FEAT)
    amp = np.exp2(np.random.uniform(-9.0, 1.0, (B, 1, 1, T)))
    return {"x_real": bf(amp * (np.random.standard_normal((B, C, F, T)) + 0.6)),
            "x_imag": bf(amp * (np.random.standard_normal((B, C, F, T)) + 0.2)),
            "ln_w": bf((1.0 + 0.1 * np.random.standard_normal((NB, FEAT))) * s),
            "ln_b": bf(0.1 * np.random.standard_normal((NB, FEAT)) * s),
            "fc_w": bf(np.random.standard_normal((NB, FEAT, EMB)) / np.sqrt(FEAT) / s[:, None]),
            "fc_b": bf(0.3 * np.random.standard_normal((NB, EMB)))}


def reference(x_real, x_imag, ln_w, ln_b, fc_w, fc_b):
    x_real, x_imag, ln_w, ln_b, fc_w, fc_b = f64(x_real), f64(x_imag), f64(ln_w), f64(ln_b), f64(fc_w), f64(fc_b)
    b, c, f, t = x_real.shape
    nb, feat = ln_w.shape
    bw = f // nb
    xr = np.transpose(x_real, (0, 3, 1, 2)).reshape(b, t, c, nb, bw)
    xi = np.transpose(x_imag, (0, 3, 1, 2)).reshape(b, t, c, nb, bw)
    xb = np.stack([xr, xi], axis=-1)
    xb = np.transpose(xb, (0, 3, 1, 2, 4, 5))
    xb = xb.reshape(b, nb, t, feat)
    mean = np.mean(xb, axis=-1, keepdims=True)
    var = np.mean(np.square(xb - mean), axis=-1, keepdims=True)
    xn = (xb - mean) * (1.0 / np.sqrt(var + EPS))
    xn = xn * ln_w[None, :, None, :] + ln_b[None, :, None, :]
    z = (mxq(xn, 3, "e4m3") @ mxq(fc_w, 1, "e4m3")[None]) + fc_b[None, :, None, :]
    return z

@@ -1,0 +1,191 @@
+from contextlib import ExitStack
+
+import concourse.bass as bass
+import concourse.mybir as mybir
+import concourse.tile as tile
+from concourse.masks import make_identity
+
+F32 = mybir.dt.float32
+BF16 = mybir.dt.bfloat16
+U32 = mybir.dt.uint32
+U8 = mybir.dt.uint8
+FP8X4 = mybir.dt.float8_e4m3fn_x4
+ALU = mybir.AluOpType
+ACTF = mybir.ActivationFunctionType
+
+B, C, NB, BW, T, EMB = 4, 2, 2, 256, 1024, 512
+FEAT = C * BW * 2
+EPS = 1e-5
+P = 128
+FLOPS = 2 * B * NB * T * FEAT * EMB
+
+RG_ON_GPSIMD = False
+XS_BUFS = 6
+
+
+def regroup(nc, on_gpsimd, dst, src):
+    if on_gpsimd:
+        nc.gpsimd.tensor_scalar(
+            out=dst, in0=src.rearrange("p j c -> p c j"), scalar1=1.0, scalar2=0.0,
+            op0=ALU.mult, op1=ALU.add,
+        )
+    else:
+        nc.vector.tensor_copy(
+            out=dst.rearrange("p (c i) j -> p c j i", i=4),
+            in_=src.rearrange("p j (c i) -> p c j i", i=4),
+        )
+
+
+def tile_bandsplitmodule_t_kernel(tc, x_real, x_imag, ln_w, ln_b, fc_w, fc_b, out):
+    nc = tc.nc
+    with ExitStack() as ctx:
+        const = ctx.enter_context(tc.tile_pool(name="const", bufs=1))
+        wstage = ctx.enter_context(tc.tile_pool(name="wstage", bufs=1))
+        xpool = ctx.enter_context(tc.tile_pool(name="xpool", bufs=XS_BUFS))
+        small = ctx.enter_context(tc.tile_pool(name="small", bufs=4))
+        vpool = ctx.enter_context(tc.tile_pool(name="vpool", bufs=2))
+        ppool = ctx.enter_context(tc.tile_pool(name="ppool", bufs=2))
+        qpool = ctx.enter_context(tc.tile_pool(name="qpool", bufs=2))
+        opool = ctx.enter_context(tc.tile_pool(name="opool", bufs=4))
+        ps_x = ctx.enter_context(tc.psum_pool(name="ps_x", bufs=4))
+        ps_v = ctx.enter_context(tc.psum_pool(name="ps_v", bufs=2))
+        ps_z = ctx.enter_context(tc.psum_pool(name="ps_z", bufs=2))
+
+        zero_t = const.tile([P, 1], F32)
+        nc.vector.memset(zero_t[:], 0.0)
+        eps_t = const.tile([P, 1], F32)
+        nc.vector.tensor_scalar(out=eps_t[:], in0=zero_t[:], scalar1=EPS, scalar2=None, op0=ALU.add)
+        warm = const.tile([P, 1], F32)
+        nc.scalar.activation(out=warm[:], in_=eps_t[:], func=ACTF.Sqrt)
+        ident = const.tile([P, P], F32)
+        make_identity(nc, ident[:])
+
+        wsc = const.tile([P, NB * C * 4], F32)
+        bsc = const.tile([P, NB * C * 4], F32)
+        for n in range(NB):
+            wl = const.tile([P, C, 4], BF16, name="wl%d" % n)
+            bl = const.tile([P, C, 4], BF16, name="bl%d" % n)
+            nc.scalar.dma_start(out=wl[:], in_=ln_w[n].rearrange("(c p j) -> p c j", c=C, j=4))
+            nc.scalar.dma_start(out=bl[:], in_=ln_b[n].rearrange("(c p j) -> p c j", c=C, j=4))
+            nc.vector.tensor_copy(out=wsc[:, n * 8:(n + 1) * 8], in_=wl[:].rearrange("p c j -> p (c j)"))
+            nc.vector.tensor_copy(out=bsc[:, n * 8:(n + 1) * 8], in_=bl[:].rearrange("p c j -> p (c j)"))
+
+        bias_bf = const.tile([P, NB * EMB], BF16)
+        nc.scalar.dma_start(out=bias_bf[:], in_=fc_b.rearrange("n e -> (n e)").partition_broadcast(P))
+        bias = const.tile([P, NB * EMB], F32)
+        nc.gpsimd.tensor_copy(out=bias[:], in_=bias_bf[:])
+
+        wcodes = const.tile([P, NB * C * EMB], U32, align_bytes=64)
+        wscales = const.tile([P, NB * C * EMB], U8, align_bytes=64)
+
+        xs_tiles = {}
+
+        def load_x(i):
+            b, n = divmod(i, NB)
+            xs = xpool.tile([P, 4 * 2 * T], BF16, name="xs")
+            for c in range(C):
+                for r in range(2):
+                    src = (x_real if r == 0 else x_imag)[b, c, n * BW:(n + 1) * BW, :]
+                    o = (c * 2 + r) * 2 * T
+                    nc.sync.dma_start(out=xs[:, o:o + 2 * T], in_=src.rearrange("(p h) t -> p (h t)", h=2))
+            xs_tiles[i] = xs
+
+        def load_w(n):
+            wraw = wstage.tile([P, C, 4, EMB], BF16, name="wraw")
+            nc.sync.dma_start(out=wraw[:].rearrange("p g j e -> p g (j e)"),
+                              in_=fc_w[n].rearrange("(g p j) e -> p g (j e)", g=C, j=4))
+            wgrp = wstage.tile([P, C, EMB, 4], BF16, name="wgrp", align_bytes=64)
+            for g in range(C):
+                regroup(nc, RG_ON_GPSIMD, wgrp[:, g], wraw[:, g])
+            o = n * C * EMB
+            nc.vector.quantize_mx(
+                out=wcodes[:, o:o + C * EMB].bitcast(FP8X4),
+                scales=wscales[:, o:o + C * EMB],
+                in_=wgrp[:].rearrange("p g e j -> p (g e j)"),
+            )
+
+        load_x(0)
+        load_w(0)
+        load_x(1)
+        load_w(1)
+        for i in range(2, XS_BUFS):
+            load_x(i)
+
+        for i in range(B * NB):
+            b, n = divmod(i, NB)
+            xs = xs_tiles[i]
+            xw = xs[:].bitcast(F32)
+            for half in range(2):
+                v = vpool.tile([P, 2, 2, FEAT], F32, name="v")
+                for tbl in range(2):
+                    w0 = (half * 512 + tbl * 256) // 2
+                    st = small.tile([P, 2, 2, 6], F32, name="st")
+                    banks = []
+                    for k in range(C):
+                        xt = ps_x.tile([P, 512], F32, name="xt")
+                        for sl in range(4):
+                            h, r = divmod(sl, 2)
+                            o = ((k * 2 + r) * 2 + h) * (T // 2) + w0
+                            nc.tensor.transpose(out=xt[:, sl * P:(sl + 1) * P], in_=xw[:, o:o + P], identity=ident[:])
+                        banks.append(xt[:].bitcast(BF16).rearrange("w (q e) -> w q e", e=2))
+                    for k in range(C):
+                        for e in range(2):
+                            nc.vector.bn_stats(out=st[:, e, k, :], in_=banks[k][:, :, e])
+                    mv = small.tile([P, 2, 2], F32, name="mv")
+                    for e in range(2):
+                        nc.vector.bn_aggr(out=mv[:, e, :], in_=st[:, e].rearrange("p k s -> p (k s)"))
+                    sd = small.tile([P, 2], F32, name="sd")
+                    nc.scalar.activation(out=sd[:], in_=mv[:, :, 1], func=ACTF.Sqrt, bias=eps_t[:], scale=1.0)
+                    rs = small.tile([P, 2], F32, name="rs")
+                    nc.vector.reciprocal(out=rs[:], in_=sd[:])
+                    nm = small.tile([P, 2], F32, name="nm")
+                    nc.vector.scalar_tensor_tensor(out=nm[:], in0=mv[:, :, 0], scalar=-1.0, in1=rs[:],
+                                                   op0=ALU.mult, op1=ALU.mult)
+                    for k in range(C):
+                        for e in range(2):
+                            nc.scalar.activation(out=v[:, tbl, e, k * 512:(k + 1) * 512], in_=banks[k][:, :, e],
+                                                 func=ACTF.Identity, scale=rs[:, e:e + 1], bias=nm[:, e:e + 1])
+
+                planes = ppool.tile([P, 8, 512], BF16, name="planes")
+                grouped = ppool.tile([P, C, 512, 4], BF16, name="grouped", align_bytes=64)
+                codes = qpool.tile([P, C * 512], U32, name="codes", align_bytes=64)
+                scl = qpool.tile([P, C * 512], U8, name="scl", align_bytes=64)
+                for g in range(C):
+                    for j in range(4):
+                        s = g * 4 + j
+                        vt = ps_v.tile([P, 512], F32, name="vt")
+                        for m in range(4):
+                            tbl, e = divmod(m, 2)
+                            nc.tensor.transpose(out=vt[:, m * P:(m + 1) * P], in_=v[:, tbl, e, s * P:(s + 1) * P],
+                                                identity=ident[:])
+                        col = n * 8 + s
+                        nc.scalar.activation(out=planes[:, s, :], in_=vt[:], func=ACTF.Identity,
+                                             scale=wsc[:, col:col + 1], bias=bsc[:, col:col + 1])
+                    regroup(nc, RG_ON_GPSIMD, grouped[:, g], planes[:, g * 4:(g + 1) * 4, :])
+                    nc.vector.quantize_mx(
+                        out=codes[:, g * 512:(g + 1) * 512].bitcast(FP8X4),
+                        scales=scl[:, g * 512:(g + 1) * 512],
+                        in_=grouped[:, g].rearrange("p c j -> p (c j)"),
+                    )
+                for tbl in range(2):
+                    zo = opool.tile([P, 2, EMB], F32, name="zo")
+                    for e in range(2):
+                        m = tbl * 2 + e
+                        z = ps_z.tile([P, EMB], F32, name="z")
+                        for g in range(C):
+                            lo = g * 512 + m * P
+                            ro = (n * C + g) * EMB
+                            nc.tensor.matmul_mx(
+                                out=z[:],
+                                lhsT=codes[:, lo:lo + P].bitcast(FP8X4),
+                                lhsT_scale=scl[:, lo:lo + P],
+                                rhs=wcodes[:, ro:ro + EMB].bitcast(FP8X4),
+                                rhs_scale=wscales[:, ro:ro + EMB],
+                                start=(g == 0),
+                                stop=(g == C - 1),
+                            )
+                        nc.vector.tensor_tensor(out=zo[:, e, :], in0=z[:], in1=bias[:, n * EMB:(n + 1) * EMB], op=ALU.add)
+                    t0 = half * 512 + tbl * 256
+                    nc.sync.dma_start(out=out[b, n, t0:t0 + 256, :].rearrange("(w e) d -> w e d", e=2), in_=zo[:])
+            if i + XS_BUFS < B * NB:
+                load_x(i + XS_BUFS)

@@ -1,8 +1,6 @@
 from contextlib import ExitStack
 
-import concourse.bass as bass
 import concourse.mybir as mybir
-import concourse.tile as tile
 from concourse.masks import make_identity
 
 F32 = mybir.dt.float32
@@ -19,8 +17,11 @@ EPS = 1e-5
 P = 128
 FLOPS = 2 * B * NB * T * FEAT * EMB
 
-RG_ON_GPSIMD = False
-XS_BUFS = 6
+RG_ON_GPSIMD = True
+MANUAL = True
+XS_BUFS = 5
+NU = B * NB * 4
+NSU = NU // 2
 
 
 def regroup(nc, on_gpsimd, dst, src):
@@ -50,6 +51,49 @@ def tile_bandsplitmodule_t_kernel(tc, x_real, x_imag, ln_w, ln_b, fc_w, fc_b, ou
         ps_x = ctx.enter_context(tc.psum_pool(name="ps_x", bufs=4))
         ps_v = ctx.enter_context(tc.psum_pool(name="ps_v", bufs=2))
         ps_z = ctx.enter_context(tc.psum_pool(name="ps_z", bufs=2))
+        if MANUAL:
+            ctx.enter_context(tc.manual_schedule())
+
+        xs_tiles = {}
+        wgrps = {}
+        banks = {}
+        sts = {}
+        mvs = {}
+        sds = {}
+        rss = {}
+        nms = {}
+        vs = {}
+        pls = {}
+        grs = {}
+        cds = {}
+        scs = {}
+        vts = {}
+
+        def load_x(i, pieces):
+            b, n = divmod(i, NB)
+            xs = xpool.tile([P, 4 * 2 * T], BF16, name="xs")
+            xs_tiles[i] = xs
+            w = T // pieces
+            for q in range(pieces):
+                for c in range(C):
+                    for r in range(2):
+                        src = (x_real if r == 0 else x_imag)[b, c, n * BW:(n + 1) * BW, q * w:(q + 1) * w]
+                        o = (c * 2 + r) * 2 * T
+                        dst = xs[:, o:o + 2 * T].rearrange("p (h t) -> p h t", h=2)[:, :, q * w:(q + 1) * w]
+                        nc.sync.dma_start(out=dst, in_=src.rearrange("(p h) t -> p h t", h=2))
+
+        def load_w(n):
+            wraw = wstage.tile([P, C, 4, EMB], BF16, name="wraw%d" % n)
+            nc.sync.dma_start(out=wraw[:].rearrange("p g j e -> p g (j e)"),
+                              in_=fc_w[n].rearrange("(g p j) e -> p g (j e)", g=C, j=4))
+            return wraw
+
+        load_x(0, 4)
+        wraw0 = load_w(0)
+        load_x(1, 1)
+        wraw1 = load_w(1)
+        for i in range(2, XS_BUFS):
+            load_x(i, 1)
 
         zero_t = const.tile([P, 1], F32)
         nc.vector.memset(zero_t[:], 0.0)
@@ -67,8 +111,8 @@ def tile_bandsplitmodule_t_kernel(tc, x_real, x_imag, ln_w, ln_b, fc_w, fc_b, ou
             bl = const.tile([P, C, 4], BF16, name="bl%d" % n)
             nc.scalar.dma_start(out=wl[:], in_=ln_w[n].rearrange("(c p j) -> p c j", c=C, j=4))
             nc.scalar.dma_start(out=bl[:], in_=ln_b[n].rearrange("(c p j) -> p c j", c=C, j=4))
-            nc.vector.tensor_copy(out=wsc[:, n * 8:(n + 1) * 8], in_=wl[:].rearrange("p c j -> p (c j)"))
-            nc.vector.tensor_copy(out=bsc[:, n * 8:(n + 1) * 8], in_=bl[:].rearrange("p c j -> p (c j)"))
+            nc.gpsimd.tensor_copy(out=wsc[:, n * 8:(n + 1) * 8], in_=wl[:].rearrange("p c j -> p (c j)"))
+            nc.gpsimd.tensor_copy(out=bsc[:, n * 8:(n + 1) * 8], in_=bl[:].rearrange("p c j -> p (c j)"))
 
         bias_bf = const.tile([P, NB * EMB], BF16)
         nc.scalar.dma_start(out=bias_bf[:], in_=fc_b.rearrange("n e -> (n e)").partition_broadcast(P))
@@ -77,115 +121,163 @@ def tile_bandsplitmodule_t_kernel(tc, x_real, x_imag, ln_w, ln_b, fc_w, fc_b, ou
 
         wcodes = const.tile([P, NB * C * EMB], U32, align_bytes=64)
         wscales = const.tile([P, NB * C * EMB], U8, align_bytes=64)
-
-        xs_tiles = {}
-
-        def load_x(i):
-            b, n = divmod(i, NB)
-            xs = xpool.tile([P, 4 * 2 * T], BF16, name="xs")
-            for c in range(C):
-                for r in range(2):
-                    src = (x_real if r == 0 else x_imag)[b, c, n * BW:(n + 1) * BW, :]
-                    o = (c * 2 + r) * 2 * T
-                    nc.sync.dma_start(out=xs[:, o:o + 2 * T], in_=src.rearrange("(p h) t -> p (h t)", h=2))
-            xs_tiles[i] = xs
-
-        def load_w(n):
-            wraw = wstage.tile([P, C, 4, EMB], BF16, name="wraw")
-            nc.sync.dma_start(out=wraw[:].rearrange("p g j e -> p g (j e)"),
-                              in_=fc_w[n].rearrange("(g p j) e -> p g (j e)", g=C, j=4))
-            wgrp = wstage.tile([P, C, EMB, 4], BF16, name="wgrp", align_bytes=64)
+        for n, wraw in ((0, wraw0), (1, wraw1)):
+            wgrp = wstage.tile([P, C, EMB, 4], BF16, name="wgrp%d" % n, align_bytes=64)
+            wgrps[n] = wgrp
             for g in range(C):
                 regroup(nc, RG_ON_GPSIMD, wgrp[:, g], wraw[:, g])
+
+        def quant_w(n):
             o = n * C * EMB
             nc.vector.quantize_mx(
                 out=wcodes[:, o:o + C * EMB].bitcast(FP8X4),
                 scales=wscales[:, o:o + C * EMB],
-                in_=wgrp[:].rearrange("p g e j -> p (g e j)"),
+                in_=wgrps[n][:].rearrange("p g e j -> p (g e j)"),
             )
 
-        load_x(0)
-        load_w(0)
-        load_x(1)
-        load_w(1)
-        for i in range(2, XS_BUFS):
-            load_x(i)
+        def t1(u):
+            i, q = divmod(u, 4)
+            xw = xs_tiles[i][:].bitcast(F32)
+            w0 = q * 128
+            bk = []
+            for k in range(C):
+                xt = ps_x.tile([P, 512], F32, name="xt")
+                for sl in range(4):
+                    h, r = divmod(sl, 2)
+                    o = ((k * 2 + r) * 2 + h) * (T // 2) + w0
+                    nc.tensor.transpose(out=xt[:, sl * P:(sl + 1) * P], in_=xw[:, o:o + P], identity=ident[:])
+                bk.append(xt[:].bitcast(BF16).rearrange("w (q e) -> w q e", e=2))
+            banks[u] = bk
+            if q == 3 and i + XS_BUFS < B * NB:
+                load_x(i + XS_BUFS, 1)
 
-        for i in range(B * NB):
+        def bn(u):
+            st = small.tile([P, 2, 2, 6], F32, name="st")
+            sts[u] = st
+            for k in range(C):
+                for e in range(2):
+                    nc.vector.bn_stats(out=st[:, e, k, :], in_=banks[u][k][:, :, e])
+
+        def aggr(u):
+            mv = small.tile([P, 2, 2], F32, name="mv")
+            mvs[u] = mv
+            for e in range(2):
+                nc.vector.bn_aggr(out=mv[:, e, :], in_=sts[u][:, e].rearrange("p k s -> p (k s)"))
+
+        def sqrt_(u):
+            sd = small.tile([P, 2], F32, name="sd")
+            sds[u] = sd
+            nc.scalar.activation(out=sd[:], in_=mvs[u][:, :, 1], func=ACTF.Sqrt, bias=eps_t[:], scale=1.0)
+
+        def rcp(u):
+            rs = small.tile([P, 2], F32, name="rs")
+            rss[u] = rs
+            nc.vector.reciprocal(out=rs[:], in_=sds[u][:])
+            nm = small.tile([P, 2], F32, name="nm")
+            nms[u] = nm
+            nc.vector.scalar_tensor_tensor(out=nm[:], in0=mvs[u][:, :, 0], scalar=-1.0, in1=rs[:],
+                                           op0=ALU.mult, op1=ALU.mult)
+
+        def p2(u):
+            su, tbl = divmod(u, 2)
+            if tbl == 0:
+                vs[su] = vpool.tile([P, 2, 2, FEAT], F32, name="v")
+            v = vs[su]
+            for k in range(C):
+                for e in range(2):
+                    nc.scalar.activation(out=v[:, tbl, e, k * 512:(k + 1) * 512], in_=banks[u][k][:, :, e],
+                                         func=ACTF.Identity, scale=rss[u][:, e:e + 1], bias=nms[u][:, e:e + 1])
+
+        def t2(su, g, j):
+            s = g * 4 + j
+            vt = ps_v.tile([P, 512], F32, name="vt")
+            vts[(su, s)] = vt
+            for m in range(4):
+                tbl, e = divmod(m, 2)
+                nc.tensor.transpose(out=vt[:, m * P:(m + 1) * P], in_=vs[su][:, tbl, e, s * P:(s + 1) * P],
+                                    identity=ident[:])
+
+        def p3(su, g, j):
+            s = g * 4 + j
+            n = (su // 2) % NB
+            if s == 0:
+                pls[su] = ppool.tile([P, 8, 512], BF16, name="planes")
+            col = n * 8 + s
+            nc.scalar.activation(out=pls[su][:, s, :], in_=vts[(su, s)][:], func=ACTF.Identity,
+                                 scale=wsc[:, col:col + 1], bias=bsc[:, col:col + 1])
+
+        def rg(su, g):
+            if g == 0:
+                grs[su] = ppool.tile([P, C, 512, 4], BF16, name="grouped", align_bytes=64)
+            regroup(nc, RG_ON_GPSIMD, grs[su][:, g], pls[su][:, g * 4:(g + 1) * 4, :])
+
+        def quant(su, g):
+            if g == 0:
+                cds[su] = qpool.tile([P, C * 512], U32, name="codes", align_bytes=64)
+                scs[su] = qpool.tile([P, C * 512], U8, name="scl", align_bytes=64)
+            nc.vector.quantize_mx(
+                out=cds[su][:, g * 512:(g + 1) * 512].bitcast(FP8X4),
+                scales=scs[su][:, g * 512:(g + 1) * 512],
+                in_=grs[su][:, g].rearrange("p c j -> p (c j)"),
+            )
+
+        def mx_ev(su, tbl):
+            i, half = divmod(su, 2)
             b, n = divmod(i, NB)
-            xs = xs_tiles[i]
-            xw = xs[:].bitcast(F32)
-            for half in range(2):
-                v = vpool.tile([P, 2, 2, FEAT], F32, name="v")
-                for tbl in range(2):
-                    w0 = (half * 512 + tbl * 256) // 2
-                    st = small.tile([P, 2, 2, 6], F32, name="st")
-                    banks = []
-                    for k in range(C):
-                        xt = ps_x.tile([P, 512], F32, name="xt")
-                        for sl in range(4):
-                            h, r = divmod(sl, 2)
-                            o = ((k * 2 + r) * 2 + h) * (T // 2) + w0
-                            nc.tensor.transpose(out=xt[:, sl * P:(sl + 1) * P], in_=xw[:, o:o + P], identity=ident[:])
-                        banks.append(xt[:].bitcast(BF16).rearrange("w (q e) -> w q e", e=2))
-                    for k in range(C):
-                        for e in range(2):
-                            nc.vector.bn_stats(out=st[:, e, k, :], in_=banks[k][:, :, e])
-                    mv = small.tile([P, 2, 2], F32, name="mv")
-                    for e in range(2):
-                        nc.vector.bn_aggr(out=mv[:, e, :], in_=st[:, e].rearrange("p k s -> p (k s)"))
-                    sd = small.tile([P, 2], F32, name="sd")
-                    nc.scalar.activation(out=sd[:], in_=mv[:, :, 1], func=ACTF.Sqrt, bias=eps_t[:], scale=1.0)
-                    rs = small.tile([P, 2], F32, name="rs")
-                    nc.vector.reciprocal(out=rs[:], in_=sd[:])
-                    nm = small.tile([P, 2], F32, name="nm")
-                    nc.vector.scalar_tensor_tensor(out=nm[:], in0=mv[:, :, 0], scalar=-1.0, in1=rs[:],
-                                                   op0=ALU.mult, op1=ALU.mult)
-                    for k in range(C):
-                        for e in range(2):
-                            nc.scalar.activation(out=v[:, tbl, e, k * 512:(k + 1) * 512], in_=banks[k][:, :, e],
-                                                 func=ACTF.Identity, scale=rs[:, e:e + 1], bias=nm[:, e:e + 1])
-
-                planes = ppool.tile([P, 8, 512], BF16, name="planes")
-                grouped = ppool.tile([P, C, 512, 4], BF16, name="grouped", align_bytes=64)
-                codes = qpool.tile([P, C * 512], U32, name="codes", align_bytes=64)
-                scl = qpool.tile([P, C * 512], U8, name="scl", align_bytes=64)
+            zs = []
+            for e in range(2):
+                m = tbl * 2 + e
+                z = ps_z.tile([P, EMB], F32, name="z")
+                zs.append(z)
                 for g in range(C):
-                    for j in range(4):
-                        s = g * 4 + j
-                        vt = ps_v.tile([P, 512], F32, name="vt")
-                        for m in range(4):
-                            tbl, e = divmod(m, 2)
-                            nc.tensor.transpose(out=vt[:, m * P:(m + 1) * P], in_=v[:, tbl, e, s * P:(s + 1) * P],
-                                                identity=ident[:])
-                        col = n * 8 + s
-                        nc.scalar.activation(out=planes[:, s, :], in_=vt[:], func=ACTF.Identity,
-                                             scale=wsc[:, col:col + 1], bias=bsc[:, col:col + 1])
-                    regroup(nc, RG_ON_GPSIMD, grouped[:, g], planes[:, g * 4:(g + 1) * 4, :])
-                    nc.vector.quantize_mx(
-                        out=codes[:, g * 512:(g + 1) * 512].bitcast(FP8X4),
-                        scales=scl[:, g * 512:(g + 1) * 512],
-                        in_=grouped[:, g].rearrange("p c j -> p (c j)"),
+                    lo = g * 512 + m * P
+                    ro = (n * C + g) * EMB
+                    nc.tensor.matmul_mx(
+                        out=z[:],
+                        lhsT=cds[su][:, lo:lo + P].bitcast(FP8X4),
+                        lhsT_scale=scs[su][:, lo:lo + P],
+                        rhs=wcodes[:, ro:ro + EMB].bitcast(FP8X4),
+                        rhs_scale=wscales[:, ro:ro + EMB],
+                        start=(g == 0),
+                        stop=(g == C - 1),
                     )
-                for tbl in range(2):
-                    zo = opool.tile([P, 2, EMB], F32, name="zo")
-                    for e in range(2):
-                        m = tbl * 2 + e
-                        z = ps_z.tile([P, EMB], F32, name="z")
-                        for g in range(C):
-                            lo = g * 512 + m * P
-                            ro = (n * C + g) * EMB
-                            nc.tensor.matmul_mx(
-                                out=z[:],
-                                lhsT=codes[:, lo:lo + P].bitcast(FP8X4),
-                                lhsT_scale=scl[:, lo:lo + P],
-                                rhs=wcodes[:, ro:ro + EMB].bitcast(FP8X4),
-                                rhs_scale=wscales[:, ro:ro + EMB],
-                                start=(g == 0),
-                                stop=(g == C - 1),
-                            )
-                        nc.vector.tensor_tensor(out=zo[:, e, :], in0=z[:], in1=bias[:, n * EMB:(n + 1) * EMB], op=ALU.add)
-                    t0 = half * 512 + tbl * 256
-                    nc.sync.dma_start(out=out[b, n, t0:t0 + 256, :].rearrange("(w e) d -> w e d", e=2), in_=zo[:])
-            if i + XS_BUFS < B * NB:
-                load_x(i + XS_BUFS)
+            zo = opool.tile([P, 2, EMB], F32, name="zo")
+            for e in range(2):
+                nc.vector.tensor_tensor(out=zo[:, e, :], in0=zs[e][:], in1=bias[:, n * EMB:(n + 1) * EMB], op=ALU.add)
+            t0 = half * 512 + tbl * 256
+            nc.sync.dma_start(out=out[b, n, t0:t0 + 256, :].rearrange("(w e) d -> w e d", e=2), in_=zo[:])
+
+        for step in range(-2, NU + 8):
+            kp, g = divmod(step - 2, 2)
+            do_p3 = 0 <= kp < NSU
+            if do_p3:
+                t2(kp, g, 0)
+                t2(kp, g, 1)
+            if 0 <= step + 1 < NU:
+                aggr(step + 1)
+            if step == 2:
+                quant_w(0)
+            if step == 3:
+                quant_w(1)
+            kq, gq = divmod(step - 4, 2)
+            if 0 <= kq < NSU:
+                quant(kq, gq)
+            km, tblm = divmod(step - 6, 2)
+            if 0 <= km < NSU:
+                mx_ev(km, tblm)
+            if 0 <= step < NU:
+                p2(step)
+            if 0 <= step + 1 < NU:
+                sqrt_(step + 1)
+                rcp(step + 1)
+            if 0 <= step + 2 < NU:
+                t1(step + 2)
+                bn(step + 2)
+            if do_p3:
+                p3(kp, g, 0)
+                t2(kp, g, 2)
+                p3(kp, g, 1)
+                t2(kp, g, 3)
+                p3(kp, g, 2)
+                p3(kp, g, 3)
+                rg(kp, g)

@@ -46,6 +46,7 @@ def tile_bandsplitmodule_t_kernel(tc, x_real, x_imag, ln_w, ln_b, fc_w, fc_b, ou
         small = ctx.enter_context(tc.tile_pool(name="small", bufs=4))
         vpool = ctx.enter_context(tc.tile_pool(name="vpool", bufs=2))
         ppool = ctx.enter_context(tc.tile_pool(name="ppool", bufs=2))
+        gpool = ctx.enter_context(tc.tile_pool(name="gpool", bufs=1))
         qpool = ctx.enter_context(tc.tile_pool(name="qpool", bufs=2))
         opool = ctx.enter_context(tc.tile_pool(name="opool", bufs=4))
         ps_x = ctx.enter_context(tc.psum_pool(name="ps_x", bufs=4))
@@ -135,20 +136,19 @@ def tile_bandsplitmodule_t_kernel(tc, x_real, x_imag, ln_w, ln_b, fc_w, fc_b, ou
                 in_=wgrps[n][:].rearrange("p g e j -> p (g e j)"),
             )
 
-        def t1(u):
+        zss = {}
+
+        def t1k(u, k):
             i, q = divmod(u, 4)
             xw = xs_tiles[i][:].bitcast(F32)
             w0 = q * 128
-            bk = []
-            for k in range(C):
-                xt = ps_x.tile([P, 512], F32, name="xt")
-                for sl in range(4):
-                    h, r = divmod(sl, 2)
-                    o = ((k * 2 + r) * 2 + h) * (T // 2) + w0
-                    nc.tensor.transpose(out=xt[:, sl * P:(sl + 1) * P], in_=xw[:, o:o + P], identity=ident[:])
-                bk.append(xt[:].bitcast(BF16).rearrange("w (q e) -> w q e", e=2))
-            banks[u] = bk
-            if q == 3 and i + XS_BUFS < B * NB:
+            xt = ps_x.tile([P, 512], F32, name="xt")
+            for sl in range(4):
+                h, r = divmod(sl, 2)
+                o = ((k * 2 + r) * 2 + h) * (T // 2) + w0
+                nc.tensor.transpose(out=xt[:, sl * P:(sl + 1) * P], in_=xw[:, o:o + P], identity=ident[:])
+            banks[(u, k)] = xt[:].bitcast(BF16).rearrange("w (q e) -> w q e", e=2)
+            if k == 1 and q == 3 and i + XS_BUFS < B * NB:
                 load_x(i + XS_BUFS, 1)
 
         def bn(u):
@@ -156,7 +156,7 @@ def tile_bandsplitmodule_t_kernel(tc, x_real, x_imag, ln_w, ln_b, fc_w, fc_b, ou
             sts[u] = st
             for k in range(C):
                 for e in range(2):
-                    nc.vector.bn_stats(out=st[:, e, k, :], in_=banks[u][k][:, :, e])
+                    nc.vector.bn_stats(out=st[:, e, k, :], in_=banks[(u, k)][:, :, e])
 
         def aggr(u):
             mv = small.tile([P, 2, 2], F32, name="mv")
@@ -178,15 +178,12 @@ def tile_bandsplitmodule_t_kernel(tc, x_real, x_imag, ln_w, ln_b, fc_w, fc_b, ou
             nc.vector.scalar_tensor_tensor(out=nm[:], in0=mvs[u][:, :, 0], scalar=-1.0, in1=rs[:],
                                            op0=ALU.mult, op1=ALU.mult)
 
-        def p2(u):
+        def p2(u, k, e):
             su, tbl = divmod(u, 2)
-            if tbl == 0:
+            if tbl == 0 and k == 0 and e == 0:
                 vs[su] = vpool.tile([P, 2, 2, FEAT], F32, name="v")
-            v = vs[su]
-            for k in range(C):
-                for e in range(2):
-                    nc.scalar.activation(out=v[:, tbl, e, k * 512:(k + 1) * 512], in_=banks[u][k][:, :, e],
-                                         func=ACTF.Identity, scale=rss[u][:, e:e + 1], bias=nms[u][:, e:e + 1])
+            nc.scalar.activation(out=vs[su][:, tbl, e, k * 512:(k + 1) * 512], in_=banks[(u, k)][:, :, e],
+                                 func=ACTF.Identity, scale=rss[u][:, e:e + 1], bias=nms[u][:, e:e + 1])
 
         def t2(su, g, j):
             s = g * 4 + j
@@ -207,9 +204,8 @@ def tile_bandsplitmodule_t_kernel(tc, x_real, x_imag, ln_w, ln_b, fc_w, fc_b, ou
                                  scale=wsc[:, col:col + 1], bias=bsc[:, col:col + 1])
 
         def rg(su, g):
-            if g == 0:
-                grs[su] = ppool.tile([P, C, 512, 4], BF16, name="grouped", align_bytes=64)
-            regroup(nc, RG_ON_GPSIMD, grs[su][:, g], pls[su][:, g * 4:(g + 1) * 4, :])
+            grs[(su, g)] = gpool.tile([P, 512, 4], BF16, name="grouped", align_bytes=64)
+            regroup(nc, RG_ON_GPSIMD, grs[(su, g)][:], pls[su][:, g * 4:(g + 1) * 4, :])
 
         def quant(su, g):
             if g == 0:
@@ -218,12 +214,11 @@ def tile_bandsplitmodule_t_kernel(tc, x_real, x_imag, ln_w, ln_b, fc_w, fc_b, ou
             nc.vector.quantize_mx(
                 out=cds[su][:, g * 512:(g + 1) * 512].bitcast(FP8X4),
                 scales=scs[su][:, g * 512:(g + 1) * 512],
-                in_=grs[su][:, g].rearrange("p c j -> p (c j)"),
+                in_=grs[(su, g)][:].rearrange("p c j -> p (c j)"),
             )
 
-        def mx_ev(su, tbl):
-            i, half = divmod(su, 2)
-            b, n = divmod(i, NB)
+        def mx(su, tbl):
+            n = (su // 2) % NB
             zs = []
             for e in range(2):
                 m = tbl * 2 + e
@@ -241,43 +236,73 @@ def tile_bandsplitmodule_t_kernel(tc, x_real, x_imag, ln_w, ln_b, fc_w, fc_b, ou
                         start=(g == 0),
                         stop=(g == C - 1),
                     )
+            zss[(su, tbl)] = zs
+
+        def ev(su, tbl):
+            i, half = divmod(su, 2)
+            b, n = divmod(i, NB)
+            zs = zss[(su, tbl)]
             zo = opool.tile([P, 2, EMB], F32, name="zo")
             for e in range(2):
                 nc.vector.tensor_tensor(out=zo[:, e, :], in0=zs[e][:], in1=bias[:, n * EMB:(n + 1) * EMB], op=ALU.add)
             t0 = half * 512 + tbl * 256
             nc.sync.dma_start(out=out[b, n, t0:t0 + 256, :].rearrange("(w e) d -> w e d", e=2), in_=zo[:])
 
-        for step in range(-2, NU + 8):
+        for step in range(-2, NU + 5):
             kp, g = divmod(step - 2, 2)
             do_p3 = 0 <= kp < NSU
+            kn, gn = divmod(step - 1, 2)
+            do_next = 0 <= kn < NSU
+            kq, gq = divmod(step - 3, 2)
+            km, tblm = divmod(step - 5, 2)
+            do_mx = 0 <= km < NSU
+            do_p2 = 0 <= step < NU
+            do_st = 0 <= step + 1 < NU
+            do_t1 = 0 <= step + 2 < NU
+
+            if do_st:
+                bn(step + 1)
             if do_p3:
-                t2(kp, g, 0)
                 t2(kp, g, 1)
-            if 0 <= step + 1 < NU:
+            if do_mx:
+                mx(km, tblm)
+            if do_p2:
+                p2(step, 0, 0)
+            if do_p3:
+                p3(kp, g, 0)
+                t2(kp, g, 2)
+            if do_p2:
+                p2(step, 0, 1)
+            if do_t1:
+                t1k(step + 2, 0)
+            if do_p3:
+                p3(kp, g, 1)
+                t2(kp, g, 3)
+            if do_st:
                 aggr(step + 1)
+            if do_mx:
+                ev(km, tblm)
+            if do_p2:
+                p2(step, 1, 0)
+            if do_st:
+                sqrt_(step + 1)
+            if do_p3:
+                p3(kp, g, 2)
+            if do_next:
+                t2(kn, gn, 0)
+            if do_p2:
+                p2(step, 1, 1)
+            if do_t1:
+                t1k(step + 2, 1)
+            if do_p3:
+                p3(kp, g, 3)
+            if do_st:
+                rcp(step + 1)
             if step == 2:
                 quant_w(0)
             if step == 3:
                 quant_w(1)
-            kq, gq = divmod(step - 4, 2)
             if 0 <= kq < NSU:
                 quant(kq, gq)
-            km, tblm = divmod(step - 6, 2)
-            if 0 <= km < NSU:
-                mx_ev(km, tblm)
-            if 0 <= step < NU:
-                p2(step)
-            if 0 <= step + 1 < NU:
-                sqrt_(step + 1)
-                rcp(step + 1)
-            if 0 <= step + 2 < NU:
-                t1(step + 2)
-                bn(step + 2)
             if do_p3:
-                p3(kp, g, 0)
-                t2(kp, g, 2)
-                p3(kp, g, 1)
-                t2(kp, g, 3)
-                p3(kp, g, 2)
-                p3(kp, g, 3)
                 rg(kp, g)

@@ -138,11 +138,15 @@ def tile_bandsplitmodule_t_kernel(tc, x_real, x_imag, ln_w, ln_b, fc_w, fc_b, ou
 
         zss = {}
 
+        def warm_pe(bank):
+            nc.tensor.matmul(out=bank[:, 0:P], lhsT=ident[:], rhs=ident[:], start=True, stop=True)
+
         def t1k(u, k):
             i, q = divmod(u, 4)
             xw = xs_tiles[i][:].bitcast(F32)
             w0 = q * 128
             xt = ps_x.tile([P, 512], F32, name="xt")
+            warm_pe(xt)
             for sl in range(4):
                 h, r = divmod(sl, 2)
                 o = ((k * 2 + r) * 2 + h) * (T // 2) + w0
@@ -189,6 +193,7 @@ def tile_bandsplitmodule_t_kernel(tc, x_real, x_imag, ln_w, ln_b, fc_w, fc_b, ou
             s = g * 4 + j
             vt = ps_v.tile([P, 512], F32, name="vt")
             vts[(su, s)] = vt
+            warm_pe(vt)
             for m in range(4):
                 tbl, e = divmod(m, 2)
                 nc.tensor.transpose(out=vt[:, m * P:(m + 1) * P], in_=vs[su][:, tbl, e, s * P:(s + 1) * P],

@@ -193,7 +193,8 @@ def tile_bandsplitmodule_t_kernel(tc, x_real, x_imag, ln_w, ln_b, fc_w, fc_b, ou
             s = g * 4 + j
             vt = ps_v.tile([P, 512], F32, name="vt")
             vts[(su, s)] = vt
-            warm_pe(vt)
+            if j in (0, 3):
+                warm_pe(vt)
             for m in range(4):
                 tbl, e = divmod(m, 2)
                 nc.tensor.transpose(out=vt[:, m * P:(m + 1) * P], in_=vs[su][:, tbl, e, s * P:(s + 1) * P],

@@ -24,10 +24,10 @@ NU = B * NB * 4
 NSU = NU // 2
 
 
-def regroup(nc, on_gpsimd, dst, src):
+def regroup(nc, on_gpsimd, dst, src, one=1.0):
     if on_gpsimd:
         nc.gpsimd.tensor_scalar(
-            out=dst, in0=src.rearrange("p j c -> p c j"), scalar1=1.0, scalar2=0.0,
+            out=dst, in0=src.rearrange("p j c -> p c j"), scalar1=one, scalar2=0.0,
             op0=ALU.mult, op1=ALU.add,
         )
     else:
@@ -57,6 +57,7 @@ def tile_bandsplitmodule_t_kernel(tc, x_real, x_imag, ln_w, ln_b, fc_w, fc_b, ou
 
         xs_tiles = {}
         wgrps = {}
+        wraws = {}
         banks = {}
         sts = {}
         mvs = {}
@@ -70,12 +71,13 @@ def tile_bandsplitmodule_t_kernel(tc, x_real, x_imag, ln_w, ln_b, fc_w, fc_b, ou
         scs = {}
         vts = {}
 
-        def load_x(i, pieces):
+        def load_x(i, pieces, first=0, last=None):
             b, n = divmod(i, NB)
-            xs = xpool.tile([P, 4 * 2 * T], BF16, name="xs")
-            xs_tiles[i] = xs
+            if first == 0:
+                xs_tiles[i] = xpool.tile([P, 4 * 2 * T], BF16, name="xs")
+            xs = xs_tiles[i]
             w = T // pieces
-            for q in range(pieces):
+            for q in range(first, pieces if last is None else last):
                 for c in range(C):
                     for r in range(2):
                         src = (x_real if r == 0 else x_imag)[b, c, n * BW:(n + 1) * BW, q * w:(q + 1) * w]
@@ -89,9 +91,19 @@ def tile_bandsplitmodule_t_kernel(tc, x_real, x_imag, ln_w, ln_b, fc_w, fc_b, ou
                               in_=fc_w[n].rearrange("(g p j) e -> p g (j e)", g=C, j=4))
             return wraw
 
-        load_x(0, 4)
+        load_x(0, 4, 0, 2)
+        wls = {}
+        bls = {}
+        for n in range(NB):
+            wls[n] = const.tile([P, C, 4], BF16, name="wl%d" % n)
+            bls[n] = const.tile([P, C, 4], BF16, name="bl%d" % n)
+            nc.sync.dma_start(out=wls[n][:], in_=ln_w[n].rearrange("(c p j) -> p c j", c=C, j=4))
+            nc.sync.dma_start(out=bls[n][:], in_=ln_b[n].rearrange("(c p j) -> p c j", c=C, j=4))
+        load_x(0, 4, 2, 4)
         wraw0 = load_w(0)
         load_x(1, 1)
+        bias_bf = const.tile([P, NB * EMB], BF16)
+        nc.sync.dma_start(out=bias_bf[:], in_=fc_b.rearrange("n e -> (n e)").partition_broadcast(P))
         wraw1 = load_w(1)
         for i in range(2, XS_BUFS):
             load_x(i, 1)
@@ -107,26 +119,13 @@ def tile_bandsplitmodule_t_kernel(tc, x_real, x_imag, ln_w, ln_b, fc_w, fc_b, ou
 
         wsc = const.tile([P, NB * C * 4], F32)
         bsc = const.tile([P, NB * C * 4], F32)
-        for n in range(NB):
-            wl = const.tile([P, C, 4], BF16, name="wl%d" % n)
-            bl = const.tile([P, C, 4], BF16, name="bl%d" % n)
-            nc.scalar.dma_start(out=wl[:], in_=ln_w[n].rearrange("(c p j) -> p c j", c=C, j=4))
-            nc.scalar.dma_start(out=bl[:], in_=ln_b[n].rearrange("(c p j) -> p c j", c=C, j=4))
-            nc.gpsimd.tensor_copy(out=wsc[:, n * 8:(n + 1) * 8], in_=wl[:].rearrange("p c j -> p (c j)"))
-            nc.gpsimd.tensor_copy(out=bsc[:, n * 8:(n + 1) * 8], in_=bl[:].rearrange("p c j -> p (c j)"))
-
-        bias_bf = const.tile([P, NB * EMB], BF16)
-        nc.scalar.dma_start(out=bias_bf[:], in_=fc_b.rearrange("n e -> (n e)").partition_broadcast(P))
-        bias = const.tile([P, NB * EMB], F32)
-        nc.gpsimd.tensor_copy(out=bias[:], in_=bias_bf[:])
 
         wcodes = const.tile([P, NB * C * EMB], U32, align_bytes=64)
         wscales = const.tile([P, NB * C * EMB], U8, align_bytes=64)
         for n, wraw in ((0, wraw0), (1, wraw1)):
             wgrp = wstage.tile([P, C, EMB, 4], BF16, name="wgrp%d" % n, align_bytes=64)
             wgrps[n] = wgrp
-            for g in range(C):
-                regroup(nc, RG_ON_GPSIMD, wgrp[:, g], wraw[:, g])
+            wraws[n] = wraw
 
         def quant_w(n):
             o = n * C * EMB
@@ -250,7 +249,7 @@ def tile_bandsplitmodule_t_kernel(tc, x_real, x_imag, ln_w, ln_b, fc_w, fc_b, ou
             zs = zss[(su, tbl)]
             zo = opool.tile([P, 2, EMB], F32, name="zo")
             for e in range(2):
-                nc.vector.tensor_tensor(out=zo[:, e, :], in0=zs[e][:], in1=bias[:, n * EMB:(n + 1) * EMB], op=ALU.add)
+                nc.vector.tensor_tensor(out=zo[:, e, :], in0=zs[e][:], in1=bias_bf[:, n * EMB:(n + 1) * EMB], op=ALU.add)
             t0 = half * 512 + tbl * 256
             nc.sync.dma_start(out=out[b, n, t0:t0 + 256, :].rearrange("(w e) d -> w e d", e=2), in_=zo[:])
 
@@ -304,9 +303,19 @@ def tile_bandsplitmodule_t_kernel(tc, x_real, x_imag, ln_w, ln_b, fc_w, fc_b, ou
                 p3(kp, g, 3)
             if do_st:
                 rcp(step + 1)
+            if step == 0:
+                for n in range(NB):
+                    nc.vector.tensor_copy(out=wsc[:, n * 8:(n + 1) * 8], in_=wls[n][:].rearrange("p c j -> p (c j)"))
+                    nc.vector.tensor_copy(out=bsc[:, n * 8:(n + 1) * 8], in_=bls[n][:].rearrange("p c j -> p (c j)"))
+            if step in (0, 1):
+                gate = const.tile([P, 1], F32, name="gate%d" % step)
+                nc.vector.memset(gate[:], 1.0)
+                regroup(nc, True, wgrps[0][:, step], wraws[0][:, step], one=gate[:, 0:1])
             if step == 2:
                 quant_w(0)
-            if step == 3:
+            if step in (3, 4):
+                regroup(nc, False, wgrps[1][:, step - 3], wraws[1][:, step - 3])
+            if step == 5:
                 quant_w(1)
             if 0 <= kq < NSU:
                 quant(kq, gq)

@@ -113,7 +113,7 @@ def tile_bandsplitmodule_t_kernel(tc, x_real, x_imag, ln_w, ln_b, fc_w, fc_b, ou
         eps_t = const.tile([P, 1], F32)
         nc.vector.tensor_scalar(out=eps_t[:], in0=zero_t[:], scalar1=EPS, scalar2=None, op0=ALU.add)
         warm = const.tile([P, 1], F32)
-        nc.scalar.activation(out=warm[:], in_=eps_t[:], func=ACTF.Sqrt)
+        nc.scalar.activation(out=warm[:], in_=eps_t[:], func=ACTF.Abs_reciprocal_sqrt)
         ident = const.tile([P, P], F32)
         make_identity(nc, ident[:])
 
@@ -168,17 +168,14 @@ def tile_bandsplitmodule_t_kernel(tc, x_real, x_imag, ln_w, ln_b, fc_w, fc_b, ou
                 nc.vector.bn_aggr(out=mv[:, e, :], in_=sts[u][:, e].rearrange("p k s -> p (k s)"))
 
         def sqrt_(u):
-            sd = small.tile([P, 2], F32, name="sd")
-            sds[u] = sd
-            nc.scalar.activation(out=sd[:], in_=mvs[u][:, :, 1], func=ACTF.Sqrt, bias=eps_t[:], scale=1.0)
-
-        def rcp(u):
             rs = small.tile([P, 2], F32, name="rs")
             rss[u] = rs
-            nc.vector.reciprocal(out=rs[:], in_=sds[u][:])
+            nc.scalar.activation(out=rs[:], in_=mvs[u][:, :, 1], func=ACTF.Abs_reciprocal_sqrt, bias=eps_t[:], scale=1.0)
+
+        def rcp(u):
             nm = small.tile([P, 2], F32, name="nm")
             nms[u] = nm
-            nc.vector.scalar_tensor_tensor(out=nm[:], in0=mvs[u][:, :, 0], scalar=-1.0, in1=rs[:],
+            nc.vector.scalar_tensor_tensor(out=nm[:], in0=mvs[u][:, :, 0], scalar=-1.0, in1=rss[u][:],
                                            op0=ALU.mult, op1=ALU.mult)
 
         def p2(u, k, e):

@@ -20,6 +20,10 @@ FLOPS = 2 * B * NB * T * FEAT * EMB
 RG_ON_GPSIMD = True
 MANUAL = True
 XS_BUFS = 5
+GRAM = set(range(7, 32, 2))
+GN = set(range(7, 32, 2))
+VS = {u: (1, 2) if u < 4 else ((2,) if u % 2 == 0 and u >= 6 else ()) for u in range(0, 30)}
+DUM = (1, 1, 1, 1)
 NU = B * NB * 4
 NSU = NU // 2
 
@@ -70,6 +74,10 @@ def tile_bandsplitmodule_t_kernel(tc, x_real, x_imag, ln_w, ln_b, fc_w, fc_b, ou
         cds = {}
         scs = {}
         vts = {}
+        xts = {}
+        grams = {}
+        xcs = {}
+        ex2s = {}
 
         def load_x(i, pieces, first=0, last=None):
             b, n = divmod(i, NB)
@@ -117,6 +125,9 @@ def tile_bandsplitmodule_t_kernel(tc, x_real, x_imag, ln_w, ln_b, fc_w, fc_b, ou
         ident = const.tile([P, P], F32)
         make_identity(nc, ident[:])
 
+        ones_bf = const.tile([P, 2], BF16)
+        nc.vector.memset(ones_bf[:], 1.0)
+        cpool = ctx.enter_context(tc.tile_pool(name="cpool", bufs=2))
         wsc = const.tile([P, NB * C * 4], F32)
         bsc = const.tile([P, NB * C * 4], F32)
 
@@ -136,6 +147,7 @@ def tile_bandsplitmodule_t_kernel(tc, x_real, x_imag, ln_w, ln_b, fc_w, fc_b, ou
             )
 
         zss = {}
+        zos = {}
 
         def warm_pe(bank):
             nc.tensor.matmul(out=bank[:, 0:P], lhsT=ident[:], rhs=ident[:], start=True, stop=True)
@@ -145,26 +157,27 @@ def tile_bandsplitmodule_t_kernel(tc, x_real, x_imag, ln_w, ln_b, fc_w, fc_b, ou
             xw = xs_tiles[i][:].bitcast(F32)
             w0 = q * 128
             xt = ps_x.tile([P, 512], F32, name="xt")
-            warm_pe(xt)
+            if u not in GRAM and DUM[k]:
+                warm_pe(xt)
             for sl in range(4):
                 h, r = divmod(sl, 2)
                 o = ((k * 2 + r) * 2 + h) * (T // 2) + w0
                 nc.tensor.transpose(out=xt[:, sl * P:(sl + 1) * P], in_=xw[:, o:o + P], identity=ident[:])
             banks[(u, k)] = xt[:].bitcast(BF16).rearrange("w (q e) -> w q e", e=2)
+            xts[(u, k)] = xt
             if k == 1 and q == 3 and i + XS_BUFS < B * NB:
                 load_x(i + XS_BUFS, 1)
 
-        def bn(u):
-            st = small.tile([P, 2, 2, 6], F32, name="st")
-            sts[u] = st
-            for k in range(C):
-                for e in range(2):
-                    nc.vector.bn_stats(out=st[:, e, k, :], in_=banks[(u, k)][:, :, e])
+        def bn(u, k, e):
+            if k == 0 and e == 0:
+                sts[u] = small.tile([P, 2, 2, 6], F32, name="st")
+            nc.vector.bn_stats(out=sts[u][:, e, k, :], in_=banks[(u, k)][:, :, e])
 
         def aggr(u):
-            mv = small.tile([P, 2, 2], F32, name="mv")
-            mvs[u] = mv
-            for e in range(2):
+            if u not in GRAM:
+                mvs[u] = small.tile([P, 2, 2], F32, name="mv")
+            mv = mvs[u]
+            for e in range(1 if u in GRAM else 2):
                 nc.vector.bn_aggr(out=mv[:, e, :], in_=sts[u][:, e].rearrange("p k s -> p (k s)"))
 
         def sqrt_(u):
@@ -172,11 +185,53 @@ def tile_bandsplitmodule_t_kernel(tc, x_real, x_imag, ln_w, ln_b, fc_w, fc_b, ou
             rss[u] = rs
             nc.scalar.activation(out=rs[:], in_=mvs[u][:, :, 1], func=ACTF.Abs_reciprocal_sqrt, bias=eps_t[:], scale=1.0)
 
+        def gram(u):
+            i, q = divmod(u, 4)
+            xs = xs_tiles[i]
+            gb = ps_z.tile([P, EMB], F32, name="z")
+            grams[u] = gb
+            for ph in range(2):
+                for s in range(8):
+                    xe = xs[:, s * T + q * 256 + 1:s * T + (q + 1) * 256:2]
+                    if ph == 0:
+                        nc.tensor.matmul(out=gb[:, 0:P], lhsT=xe, rhs=xe, start=(s == 0), stop=(s == 7))
+                    else:
+                        nc.tensor.matmul(out=gb[:, P:P + 2], lhsT=xe, rhs=ones_bf[:], start=(s == 0), stop=(s == 7))
+
+        def diag(u):
+            gb = grams[u]
+            mvs[u] = small.tile([P, 2, 2], F32, name="mv")
+            mv = mvs[u]
+            ex2 = small.tile([P, 1], F32, name="ex2")
+            mq = small.tile([P, 1], F32, name="mq")
+            junk = small.tile([P, P], F32, name="junk")
+            nc.vector.scalar_tensor_tensor(out=junk[:], in0=gb[:, 0:P], scalar=1.0 / FEAT, in1=ident[:], op0=ALU.mult,
+                                           op1=ALU.mult, accum_out=ex2[:])
+            nc.vector.tensor_scalar(out=mq[:], in0=gb[:, P:P + 1], scalar1=-1.0 / FEAT / FEAT, scalar2=None, op0=ALU.mult)
+            nc.vector.tensor_scalar(out=mv[:, 1, 0:1], in0=gb[:, P:P + 1], scalar1=1.0 / FEAT, scalar2=None, op0=ALU.mult)
+            ex2s[u] = (ex2, mq)
+
+        def diag2(u):
+            ex2, mq = ex2s[u]
+            nc.vector.scalar_tensor_tensor(out=mvs[u][:, 1, 1:2], in0=grams[u][:, P:P + 1], scalar=mq[:], in1=ex2[:],
+                                           op0=ALU.mult, op1=ALU.add)
+
+        def p2copy(u, k):
+            xcs[(u, k)] = cpool.tile([P, 512], F32, name="xc")
+            nc.scalar.copy(out=xcs[(u, k)][:], in_=xts[(u, k)][:])
+
+        def p2g(u, k, e):
+            su, tbl = divmod(u, 2)
+            nc.gpsimd.tensor_scalar(out=vs[su][:, tbl, e, k * 512:(k + 1) * 512],
+                                    in0=xcs[(u, k)][:].bitcast(BF16).rearrange("w (q e) -> w q e", e=2)[:, :, e],
+                                    scalar1=mvs[u][:, e, 0:1], scalar2=rss[u][:, e:e + 1], op0=ALU.subtract, op1=ALU.mult)
+
         def rcp(u):
             nm = small.tile([P, 2], F32, name="nm")
             nms[u] = nm
-            nc.vector.scalar_tensor_tensor(out=nm[:], in0=mvs[u][:, :, 0], scalar=-1.0, in1=rss[u][:],
-                                           op0=ALU.mult, op1=ALU.mult)
+            for e in range(2):
+                nc.vector.tensor_scalar(out=nm[:, e:e + 1], in0=mvs[u][:, e, 0:1], scalar1=rss[u][:, e:e + 1], scalar2=-1.0,
+                                        op0=ALU.mult, op1=ALU.mult)
 
         def p2(u, k, e):
             su, tbl = divmod(u, 2)
@@ -185,11 +240,15 @@ def tile_bandsplitmodule_t_kernel(tc, x_real, x_imag, ln_w, ln_b, fc_w, fc_b, ou
             nc.scalar.activation(out=vs[su][:, tbl, e, k * 512:(k + 1) * 512], in_=banks[(u, k)][:, :, e],
                                  func=ACTF.Identity, scale=rss[u][:, e:e + 1], bias=nms[u][:, e:e + 1])
 
-        def t2(su, g, j):
+        def t2(su, g, j, spare=False):
             s = g * 4 + j
-            vt = ps_v.tile([P, 512], F32, name="vt")
+            if spare:
+                vt = ps_x.tile([P, 512], F32, name="xt")
+            else:
+                vt = ps_v.tile([P, 512], F32, name="vt")
             vts[(su, s)] = vt
-            if j in (0, 3):
+            uu = 2 * su + g + 4 if j else 2 * su + g + 3
+            if ((j == 0 and DUM[3]) or (j == 3 and DUM[2])) and uu not in GRAM:
                 warm_pe(vt)
             for m in range(4):
                 tbl, e = divmod(m, 2)
@@ -202,8 +261,24 @@ def tile_bandsplitmodule_t_kernel(tc, x_real, x_imag, ln_w, ln_b, fc_w, fc_b, ou
             if s == 0:
                 pls[su] = ppool.tile([P, 8, 512], BF16, name="planes")
             col = n * 8 + s
-            nc.scalar.activation(out=pls[su][:, s, :], in_=vts[(su, s)][:], func=ACTF.Identity,
-                                 scale=wsc[:, col:col + 1], bias=bsc[:, col:col + 1])
+            if j in VS.get(su * 2 + g, ()):
+                nc.vector.tensor_scalar(out=pls[su][:, s, :], in0=vts[(su, s)][:], scalar1=wsc[:, col:col + 1],
+                                        scalar2=bsc[:, col:col + 1], op0=ALU.mult, op1=ALU.add)
+            else:
+                nc.scalar.activation(out=pls[su][:, s, :], in_=vts[(su, s)][:], func=ACTF.Identity,
+                                     scale=wsc[:, col:col + 1], bias=bsc[:, col:col + 1])
+
+        def p3v(su, g, j):
+            s = g * 4 + j
+            if s == 0:
+                pls[su] = ppool.tile([P, 8, 512], BF16, name="planes")
+            col = ((su // 2) % NB) * 8 + s
+            nc.vector.tensor_scalar(out=pls[su][:, s, :], in0=vts[(su, s)][:], scalar1=wsc[:, col:col + 1],
+                                    scalar2=bsc[:, col:col + 1], op0=ALU.mult, op1=ALU.add)
+
+        def rg_last(su, g):
+            grs[(su, g)] = gpool.tile([P, 512, 4], BF16, name="grouped_last", align_bytes=64)
+            nc.scalar.copy(out=grs[(su, g)][:], in_=pls[su][:, g * 4:(g + 1) * 4, :].rearrange("p j c -> p c j"))
 
         def rg(su, g):
             grs[(su, g)] = gpool.tile([P, 512, 4], BF16, name="grouped", align_bytes=64)
@@ -219,38 +294,37 @@ def tile_bandsplitmodule_t_kernel(tc, x_real, x_imag, ln_w, ln_b, fc_w, fc_b, ou
                 in_=grs[(su, g)][:].rearrange("p c j -> p (c j)"),
             )
 
-        def mx(su, tbl):
+        def mx(su, tbl, e):
             n = (su // 2) % NB
-            zs = []
-            for e in range(2):
-                m = tbl * 2 + e
-                z = ps_z.tile([P, EMB], F32, name="z")
-                zs.append(z)
-                for g in range(C):
-                    lo = g * 512 + m * P
-                    ro = (n * C + g) * EMB
-                    nc.tensor.matmul_mx(
-                        out=z[:],
-                        lhsT=cds[su][:, lo:lo + P].bitcast(FP8X4),
-                        lhsT_scale=scs[su][:, lo:lo + P],
-                        rhs=wcodes[:, ro:ro + EMB].bitcast(FP8X4),
-                        rhs_scale=wscales[:, ro:ro + EMB],
-                        start=(g == 0),
-                        stop=(g == C - 1),
-                    )
-            zss[(su, tbl)] = zs
+            m = tbl * 2 + e
+            z = ps_z.tile([P, EMB], F32, name="z")
+            zss[(su, tbl, e)] = z
+            for g in range(C):
+                lo = g * 512 + m * P
+                ro = (n * C + g) * EMB
+                nc.tensor.matmul_mx(
+                    out=z[:],
+                    lhsT=cds[su][:, lo:lo + P].bitcast(FP8X4),
+                    lhsT_scale=scs[su][:, lo:lo + P],
+                    rhs=wcodes[:, ro:ro + EMB].bitcast(FP8X4),
+                    rhs_scale=wscales[:, ro:ro + EMB],
+                    start=(g == 0),
+                    stop=(g == C - 1),
+                )
 
-        def ev(su, tbl):
+        def ev(su, tbl, e):
             i, half = divmod(su, 2)
             b, n = divmod(i, NB)
-            zs = zss[(su, tbl)]
-            zo = opool.tile([P, 2, EMB], F32, name="zo")
-            for e in range(2):
-                nc.vector.tensor_tensor(out=zo[:, e, :], in0=zs[e][:], in1=bias_bf[:, n * EMB:(n + 1) * EMB], op=ALU.add)
-            t0 = half * 512 + tbl * 256
-            nc.sync.dma_start(out=out[b, n, t0:t0 + 256, :].rearrange("(w e) d -> w e d", e=2), in_=zo[:])
+            if e == 0:
+                zos[(su, tbl)] = opool.tile([P, 2, EMB], F32, name="zo")
+            zo = zos[(su, tbl)]
+            nc.vector.tensor_tensor(out=zo[:, e, :], in0=zss[(su, tbl, e)][:], in1=bias_bf[:, n * EMB:(n + 1) * EMB],
+                                    op=ALU.add)
+            if e == 1:
+                t0 = half * 512 + tbl * 256
+                nc.sync.dma_start(out=out[b, n, t0:t0 + 256, :].rearrange("(w e) d -> w e d", e=2), in_=zo[:])
 
-        for step in range(-2, NU + 5):
+        for step in range(-2, NU - 1):
             kp, g = divmod(step - 2, 2)
             do_p3 = 0 <= kp < NSU
             kn, gn = divmod(step - 1, 2)
@@ -262,59 +336,149 @@ def tile_bandsplitmodule_t_kernel(tc, x_real, x_imag, ln_w, ln_b, fc_w, fc_b, ou
             do_st = 0 <= step + 1 < NU
             do_t1 = 0 <= step + 2 < NU
 
+            gu = do_st and step + 1 in GRAM
+            gc = do_p2 and step in GN
+            if gu:
+                diag(step + 1)
             if do_st:
-                bn(step + 1)
+                bn(step + 1, 0, 0)
+            if gu:
+                diag2(step + 1)
+            elif do_st:
+                bn(step + 1, 0, 1)
+            if do_st:
+                bn(step + 1, 1, 0)
+            if do_st and not gu:
+                bn(step + 1, 1, 1)
             if do_p3:
                 t2(kp, g, 1)
             if do_mx:
-                mx(km, tblm)
+                mx(km, tblm, 0)
+                mx(km, tblm, 1)
+            if do_p3:
+                p3(kp, g, 0)
             if do_p2:
                 p2(step, 0, 0)
             if do_p3:
-                p3(kp, g, 0)
                 t2(kp, g, 2)
+            if do_mx:
+                ev(km, tblm, 0)
+            if do_p3:
+                p3(kp, g, 1)
+            if do_st:
+                aggr(step + 1)
             if do_p2:
                 p2(step, 0, 1)
             if do_t1:
                 t1k(step + 2, 0)
+            if do_mx and (gu or not do_st):
+                ev(km, tblm, 1)
             if do_p3:
-                p3(kp, g, 1)
                 t2(kp, g, 3)
-            if do_st:
-                aggr(step + 1)
-            if do_mx:
-                ev(km, tblm)
-            if do_p2:
+            if gc:
+                p2copy(step, 1)
+            elif do_p2:
                 p2(step, 1, 0)
+            if do_t1 and step + 2 in GRAM:
+                gram(step + 2)
             if do_st:
                 sqrt_(step + 1)
             if do_p3:
                 p3(kp, g, 2)
+            if do_p2 and step - 1 in GN:
+                p2g(step - 1, 1, 1)
             if do_next:
                 t2(kn, gn, 0)
-            if do_p2:
+            if do_p2 and not gc:
                 p2(step, 1, 1)
             if do_t1:
                 t1k(step + 2, 1)
             if do_p3:
                 p3(kp, g, 3)
-            if do_st:
-                rcp(step + 1)
+            if gc:
+                p2g(step, 1, 0)
             if step == 0:
                 for n in range(NB):
                     nc.vector.tensor_copy(out=wsc[:, n * 8:(n + 1) * 8], in_=wls[n][:].rearrange("p c j -> p (c j)"))
                     nc.vector.tensor_copy(out=bsc[:, n * 8:(n + 1) * 8], in_=bls[n][:].rearrange("p c j -> p (c j)"))
-            if step in (0, 1):
-                gate = const.tile([P, 1], F32, name="gate%d" % step)
+            if step in (0, 0 + 1):
+                gate = const.tile([P, 1], F32, name="gate%d" % (step - (0)))
                 nc.vector.memset(gate[:], 1.0)
-                regroup(nc, True, wgrps[0][:, step], wraws[0][:, step], one=gate[:, 0:1])
+                regroup(nc, True, wgrps[0][:, step - (0)], wraws[0][:, step - (0)], one=gate[:, 0:1])
             if step == 2:
                 quant_w(0)
-            if step in (3, 4):
-                regroup(nc, False, wgrps[1][:, step - 3], wraws[1][:, step - 3])
-            if step == 5:
+            if 3 <= step < 3 + 4:
+                q = step - 3
+                lo = (q % 2) * 256
+                regroup(nc, True, wgrps[1][:, q // 2, lo:lo + 256], wraws[1][:, q // 2, :, lo:lo + 256])
+            if step == 7:
                 quant_w(1)
             if 0 <= kq < NSU:
                 quant(kq, gq)
             if do_p3:
                 rg(kp, g)
+            if do_st:
+                rcp(step + 1)
+            if do_mx and not (gu or not do_st):
+                ev(km, tblm, 1)
+
+        u = NU - 1
+        su = NSU - 1
+        t2(su - 1, 1, 1)
+        mx(su - 2, 0, 0)
+        mx(su - 2, 0, 1)
+        p2(u, 0, 0)
+        p3(su - 1, 1, 0)
+        t2(su - 1, 1, 2)
+        p3v(su - 1, 1, 1)
+        p2(u, 0, 1)
+        t2(su - 1, 1, 3)
+        ev(su - 2, 0, 0)
+        ev(su - 2, 0, 1)
+        p3(su - 1, 1, 2)
+        t2(su, 0, 0)
+        p2(u, 1, 0)
+        p3v(su - 1, 1, 3)
+        t2(su, 0, 1)
+        p2(u, 1, 1)
+        t2(su, 0, 2, spare=True)
+        t2(su, 0, 3, spare=True)
+        quant(su - 1, 0)
+        rg(su - 1, 1)
+        p3(su, 0, 0)
+        p3v(su, 0, 1)
+        t2(su, 1, 0)
+        t2(su, 1, 1)
+        p3(su, 0, 2)
+        p3v(su, 0, 3)
+        t2(su, 1, 2, spare=True)
+        t2(su, 1, 3, spare=True)
+        p3(su, 1, 0)
+        p3v(su, 1, 1)
+        p3(su, 1, 2)
+        quant(su - 1, 1)
+        p3(su, 1, 3)
+        rg(su, 0)
+        rg_last(su, 1)
+        mx(su - 2, 1, 0)
+        mx(su - 2, 1, 1)
+        ev(su - 2, 1, 0)
+        ev(su - 2, 1, 1)
+        mx(su - 1, 0, 0)
+        mx(su - 1, 0, 1)
+        ev(su - 1, 0, 0)
+        ev(su - 1, 0, 1)
+        mx(su - 1, 1, 0)
+        mx(su - 1, 1, 1)
+        ev(su - 1, 1, 0)
+        ev(su - 1, 1, 1)
+        quant(su, 0)
+        quant(su, 1)
+        mx(su, 0, 0)
+        mx(su, 0, 1)
+        ev(su, 0, 0)
+        ev(su, 0, 1)
+        mx(su, 1, 0)
+        mx(su, 1, 1)
+        ev(su, 1, 0)
+        ev(su, 1, 1)

@@ -224,7 +224,7 @@ def tile_bandsplitmodule_t_kernel(tc, x_real, x_imag, ln_w, ln_b, fc_w, fc_b, ou
             su, tbl = divmod(u, 2)
             nc.gpsimd.tensor_scalar(out=vs[su][:, tbl, e, k * 512:(k + 1) * 512],
                                     in0=xcs[(u, k)][:].bitcast(BF16).rearrange("w (q e) -> w q e", e=2)[:, :, e],
-                                    scalar1=mvs[u][:, e, 0:1], scalar2=rss[u][:, e:e + 1], op0=ALU.subtract, op1=ALU.mult)
+                                    scalar1=rss[u][:, e:e + 1], scalar2=nms[u][:, e:e + 1], op0=ALU.mult, op1=ALU.add)
 
         def rcp(u):
             nm = small.tile([P, 2], F32, name="nm")
@@ -468,12 +468,12 @@ def tile_bandsplitmodule_t_kernel(tc, x_real, x_imag, ln_w, ln_b, fc_w, fc_b, ou
         mx(su - 1, 0, 1)
         ev(su - 1, 0, 0)
         ev(su - 1, 0, 1)
+        quant(su, 0)
+        quant(su, 1)
         mx(su - 1, 1, 0)
         mx(su - 1, 1, 1)
         ev(su - 1, 1, 0)
         ev(su - 1, 1, 1)
-        quant(su, 0)
-        quant(su, 1)
         mx(su, 0, 0)
         mx(su, 0, 1)
         ev(su, 0, 0)

@@ -21,9 +21,7 @@ RG_ON_GPSIMD = True
 MANUAL = True
 XS_BUFS = 5
 GRAM = set(range(7, 32, 2))
-GN = set(range(7, 32, 2))
-VS = {u: (1, 2) if u < 4 else ((2,) if u % 2 == 0 and u >= 6 else ()) for u in range(0, 30)}
-DUM = (1, 1, 1, 1)
+VS = {u: (() if u % 2 == 0 else (2,)) if u >= 6 else () for u in range(0, 30)}
 NU = B * NB * 4
 NSU = NU // 2
 
@@ -74,9 +72,7 @@ def tile_bandsplitmodule_t_kernel(tc, x_real, x_imag, ln_w, ln_b, fc_w, fc_b, ou
         cds = {}
         scs = {}
         vts = {}
-        xts = {}
         grams = {}
-        xcs = {}
         ex2s = {}
 
         def load_x(i, pieces, first=0, last=None):
@@ -127,7 +123,6 @@ def tile_bandsplitmodule_t_kernel(tc, x_real, x_imag, ln_w, ln_b, fc_w, fc_b, ou
 
         ones_bf = const.tile([P, 2], BF16)
         nc.vector.memset(ones_bf[:], 1.0)
-        cpool = ctx.enter_context(tc.tile_pool(name="cpool", bufs=2))
         wsc = const.tile([P, NB * C * 4], F32)
         bsc = const.tile([P, NB * C * 4], F32)
 
@@ -157,14 +152,13 @@ def tile_bandsplitmodule_t_kernel(tc, x_real, x_imag, ln_w, ln_b, fc_w, fc_b, ou
             xw = xs_tiles[i][:].bitcast(F32)
             w0 = q * 128
             xt = ps_x.tile([P, 512], F32, name="xt")
-            if u not in GRAM and DUM[k]:
+            if u not in GRAM:
                 warm_pe(xt)
             for sl in range(4):
                 h, r = divmod(sl, 2)
                 o = ((k * 2 + r) * 2 + h) * (T // 2) + w0
                 nc.tensor.transpose(out=xt[:, sl * P:(sl + 1) * P], in_=xw[:, o:o + P], identity=ident[:])
             banks[(u, k)] = xt[:].bitcast(BF16).rearrange("w (q e) -> w q e", e=2)
-            xts[(u, k)] = xt
             if k == 1 and q == 3 and i + XS_BUFS < B * NB:
                 load_x(i + XS_BUFS, 1)
 
@@ -216,22 +210,12 @@ def tile_bandsplitmodule_t_kernel(tc, x_real, x_imag, ln_w, ln_b, fc_w, fc_b, ou
             nc.vector.scalar_tensor_tensor(out=mvs[u][:, 1, 1:2], in0=grams[u][:, P:P + 1], scalar=mq[:], in1=ex2[:],
                                            op0=ALU.mult, op1=ALU.add)
 
-        def p2copy(u, k):
-            xcs[(u, k)] = cpool.tile([P, 512], F32, name="xc")
-            nc.scalar.copy(out=xcs[(u, k)][:], in_=xts[(u, k)][:])
-
-        def p2g(u, k, e):
-            su, tbl = divmod(u, 2)
-            nc.gpsimd.tensor_scalar(out=vs[su][:, tbl, e, k * 512:(k + 1) * 512],
-                                    in0=xcs[(u, k)][:].bitcast(BF16).rearrange("w (q e) -> w q e", e=2)[:, :, e],
-                                    scalar1=rss[u][:, e:e + 1], scalar2=nms[u][:, e:e + 1], op0=ALU.mult, op1=ALU.add)
 
         def rcp(u):
             nm = small.tile([P, 2], F32, name="nm")
             nms[u] = nm
-            for e in range(2):
-                nc.vector.tensor_scalar(out=nm[:, e:e + 1], in0=mvs[u][:, e, 0:1], scalar1=rss[u][:, e:e + 1], scalar2=-1.0,
-                                        op0=ALU.mult, op1=ALU.mult)
+            nc.vector.scalar_tensor_tensor(out=nm[:], in0=mvs[u][:, :, 0], scalar=-1.0, in1=rss[u][:],
+                                           op0=ALU.mult, op1=ALU.mult)
 
         def p2(u, k, e):
             su, tbl = divmod(u, 2)
@@ -248,7 +232,7 @@ def tile_bandsplitmodule_t_kernel(tc, x_real, x_imag, ln_w, ln_b, fc_w, fc_b, ou
                 vt = ps_v.tile([P, 512], F32, name="vt")
             vts[(su, s)] = vt
             uu = 2 * su + g + 4 if j else 2 * su + g + 3
-            if ((j == 0 and DUM[3]) or (j == 3 and DUM[2])) and uu not in GRAM:
+            if j in (0, 3) and uu not in GRAM:
                 warm_pe(vt)
             for m in range(4):
                 tbl, e = divmod(m, 2)
@@ -337,7 +321,6 @@ def tile_bandsplitmodule_t_kernel(tc, x_real, x_imag, ln_w, ln_b, fc_w, fc_b, ou
             do_t1 = 0 <= step + 2 < NU
 
             gu = do_st and step + 1 in GRAM
-            gc = do_p2 and step in GN
             if gu:
                 diag(step + 1)
             if do_st:
@@ -355,48 +338,42 @@ def tile_bandsplitmodule_t_kernel(tc, x_real, x_imag, ln_w, ln_b, fc_w, fc_b, ou
             if do_mx:
                 mx(km, tblm, 0)
                 mx(km, tblm, 1)
-            if do_p3:
-                p3(kp, g, 0)
             if do_p2:
                 p2(step, 0, 0)
             if do_p3:
+                p3(kp, g, 0)
                 t2(kp, g, 2)
-            if do_mx:
-                ev(km, tblm, 0)
-            if do_p3:
-                p3(kp, g, 1)
-            if do_st:
-                aggr(step + 1)
             if do_p2:
                 p2(step, 0, 1)
             if do_t1:
                 t1k(step + 2, 0)
-            if do_mx and (gu or not do_st):
-                ev(km, tblm, 1)
             if do_p3:
+                p3(kp, g, 1)
                 t2(kp, g, 3)
-            if gc:
-                p2copy(step, 1)
-            elif do_p2:
-                p2(step, 1, 0)
+            if do_mx:
+                ev(km, tblm, 0)
+            if do_st:
+                aggr(step + 1)
+            if do_mx:
+                ev(km, tblm, 1)
             if do_t1 and step + 2 in GRAM:
                 gram(step + 2)
+            if do_p2:
+                p2(step, 1, 0)
             if do_st:
                 sqrt_(step + 1)
             if do_p3:
                 p3(kp, g, 2)
-            if do_p2 and step - 1 in GN:
-                p2g(step - 1, 1, 1)
             if do_next:
                 t2(kn, gn, 0)
-            if do_p2 and not gc:
+            if do_p2:
                 p2(step, 1, 1)
             if do_t1:
                 t1k(step + 2, 1)
             if do_p3:
                 p3(kp, g, 3)
-            if gc:
-                p2g(step, 1, 0)
+            if do_st:
+                rcp(step + 1)
             if step == 0:
                 for n in range(NB):
                     nc.vector.tensor_copy(out=wsc[:, n * 8:(n + 1) * 8], in_=wls[n][:].rearrange("p c j -> p (c j)"))
@@ -417,10 +394,6 @@ def tile_bandsplitmodule_t_kernel(tc, x_real, x_imag, ln_w, ln_b, fc_w, fc_b, ou
                 quant(kq, gq)
             if do_p3:
                 rg(kp, g)
-            if do_st:
-                rcp(step + 1)
-            if do_mx and not (gu or not do_st):
-                ev(km, tblm, 1)
 
         u = NU - 1
         su = NSU - 1

@@ -20,8 +20,8 @@ FLOPS = 2 * B * NB * T * FEAT * EMB
 RG_ON_GPSIMD = True
 MANUAL = True
 XS_BUFS = 5
-GRAM = set(range(7, 32, 2))
-VS = {u: (() if u % 2 == 0 else (2,)) if u >= 6 else () for u in range(0, 30)}
+GRAM = set(u for u in range(7, 32) if u % 2 or u % 8 == 4)
+VS = {u: (2,) if u >= 6 and u % 4 != 2 else () for u in range(0, 30)}
 NU = B * NB * 4
 NSU = NU // 2
 

@@ -21,7 +21,7 @@ RG_ON_GPSIMD = True
 MANUAL = True
 XS_BUFS = 5
 GRAM = set(u for u in range(7, 32) if u % 2 or u % 8 == 4)
-VS = {u: (2,) if u >= 6 and u % 4 != 2 else () for u in range(0, 30)}
+VS = {u: (2,) if 6 <= u < 29 and u % 4 != 2 else () for u in range(0, 30)}
 NU = B * NB * 4
 NSU = NU // 2
 
@@ -57,7 +57,7 @@ def tile_bandsplitmodule_t_kernel(tc, x_real, x_imag, ln_w, ln_b, fc_w, fc_b, ou
         if MANUAL:
             ctx.enter_context(tc.manual_schedule())
 
-        xs_tiles = {}
+        x_units = {}
         wgrps = {}
         wraws = {}
         banks = {}
@@ -75,19 +75,27 @@ def tile_bandsplitmodule_t_kernel(tc, x_real, x_imag, ln_w, ln_b, fc_w, fc_b, ou
         grams = {}
         ex2s = {}
 
-        def load_x(i, pieces, first=0, last=None):
+        def load_part(dst, b, n, c, r, t0, w):
+            src = (x_real if r == 0 else x_imag)[b, c, n * BW:(n + 1) * BW, t0:t0 + w]
+            nc.sync.dma_start(out=dst.rearrange("p (h t) -> p h t", h=2), in_=src.rearrange("(p h) t -> p h t", h=2))
+
+        def load_x(i):
             b, n = divmod(i, NB)
-            if first == 0:
-                xs_tiles[i] = xpool.tile([P, 4 * 2 * T], BF16, name="xs")
-            xs = xs_tiles[i]
-            w = T // pieces
-            for q in range(first, pieces if last is None else last):
-                for c in range(C):
-                    for r in range(2):
-                        src = (x_real if r == 0 else x_imag)[b, c, n * BW:(n + 1) * BW, q * w:(q + 1) * w]
-                        o = (c * 2 + r) * 2 * T
-                        dst = xs[:, o:o + 2 * T].rearrange("p (h t) -> p h t", h=2)[:, :, q * w:(q + 1) * w]
-                        nc.sync.dma_start(out=dst, in_=src.rearrange("(p h) t -> p h t", h=2))
+            xs = xpool.tile([P, 8 * T], BF16, name="xs")
+            for q in range(4):
+                x_units[i * 4 + q] = (xs, T, q * 256)
+            for c in range(C):
+                for r in range(2):
+                    o = (c * 2 + r) * 2 * T
+                    load_part(xs[:, o:o + 2 * T], b, n, c, r, 0, T)
+
+        def load_x0(q):
+            xq = wstage.tile([P, 8 * 256], BF16, name="xq%d" % q)
+            x_units[q] = (xq, 256, 0)
+            for c in range(C):
+                for r in range(2):
+                    o = (c * 2 + r) * 2 * 256
+                    load_part(xq[:, o:o + 512], 0, 0, c, r, q * 256, 256)
 
         def load_w(n):
             wraw = wstage.tile([P, C, 4, EMB], BF16, name="wraw%d" % n)
@@ -95,7 +103,8 @@ def tile_bandsplitmodule_t_kernel(tc, x_real, x_imag, ln_w, ln_b, fc_w, fc_b, ou
                               in_=fc_w[n].rearrange("(g p j) e -> p g (j e)", g=C, j=4))
             return wraw
 
-        load_x(0, 4, 0, 2)
+        load_x0(0)
+        load_x0(1)
         wls = {}
         bls = {}
         for n in range(NB):
@@ -103,14 +112,15 @@ def tile_bandsplitmodule_t_kernel(tc, x_real, x_imag, ln_w, ln_b, fc_w, fc_b, ou
             bls[n] = const.tile([P, C, 4], BF16, name="bl%d" % n)
             nc.sync.dma_start(out=wls[n][:], in_=ln_w[n].rearrange("(c p j) -> p c j", c=C, j=4))
             nc.sync.dma_start(out=bls[n][:], in_=ln_b[n].rearrange("(c p j) -> p c j", c=C, j=4))
-        load_x(0, 4, 2, 4)
+        load_x0(2)
+        load_x0(3)
         wraw0 = load_w(0)
-        load_x(1, 1)
+        load_x(1)
         bias_bf = const.tile([P, NB * EMB], BF16)
         nc.sync.dma_start(out=bias_bf[:], in_=fc_b.rearrange("n e -> (n e)").partition_broadcast(P))
         wraw1 = load_w(1)
-        for i in range(2, XS_BUFS):
-            load_x(i, 1)
+        for i in range(2, 1 + XS_BUFS):
+            load_x(i)
 
         zero_t = const.tile([P, 1], F32)
         nc.vector.memset(zero_t[:], 0.0)
@@ -149,18 +159,18 @@ def tile_bandsplitmodule_t_kernel(tc, x_real, x_imag, ln_w, ln_b, fc_w, fc_b, ou
 
         def t1k(u, k):
             i, q = divmod(u, 4)
-            xw = xs_tiles[i][:].bitcast(F32)
-            w0 = q * 128
+            xt_in, span, t0 = x_units[u]
+            xw = xt_in[:].bitcast(F32)
             xt = ps_x.tile([P, 512], F32, name="xt")
             if u not in GRAM:
                 warm_pe(xt)
             for sl in range(4):
                 h, r = divmod(sl, 2)
-                o = ((k * 2 + r) * 2 + h) * (T // 2) + w0
+                o = (((k * 2 + r) * 2 + h) * span + t0) // 2
                 nc.tensor.transpose(out=xt[:, sl * P:(sl + 1) * P], in_=xw[:, o:o + P], identity=ident[:])
             banks[(u, k)] = xt[:].bitcast(BF16).rearrange("w (q e) -> w q e", e=2)
-            if k == 1 and q == 3 and i + XS_BUFS < B * NB:
-                load_x(i + XS_BUFS, 1)
+            if k == 1 and q == 3 and i > 0 and i + XS_BUFS < B * NB:
+                load_x(i + XS_BUFS)
 
         def bn(u, k, e):
             if k == 0 and e == 0:
@@ -180,13 +190,12 @@ def tile_bandsplitmodule_t_kernel(tc, x_real, x_imag, ln_w, ln_b, fc_w, fc_b, ou
             nc.scalar.activation(out=rs[:], in_=mvs[u][:, :, 1], func=ACTF.Abs_reciprocal_sqrt, bias=eps_t[:], scale=1.0)
 
         def gram(u):
-            i, q = divmod(u, 4)
-            xs = xs_tiles[i]
+            xs, span, t0 = x_units[u]
             gb = ps_z.tile([P, EMB], F32, name="z")
             grams[u] = gb
             for ph in range(2):
                 for s in range(8):
-                    xe = xs[:, s * T + q * 256 + 1:s * T + (q + 1) * 256:2]
+                    xe = xs[:, s * span + t0 + 1:s * span + t0 + 256:2]
                     if ph == 0:
                         nc.tensor.matmul(out=gb[:, 0:P], lhsT=xe, rhs=xe, start=(s == 0), stop=(s == 7))
                     else:
@@ -260,9 +269,27 @@ def tile_bandsplitmodule_t_kernel(tc, x_real, x_imag, ln_w, ln_b, fc_w, fc_b, ou
             nc.vector.tensor_scalar(out=pls[su][:, s, :], in0=vts[(su, s)][:], scalar1=wsc[:, col:col + 1],
                                     scalar2=bsc[:, col:col + 1], op0=ALU.mult, op1=ALU.add)
 
-        def rg_last(su, g):
-            grs[(su, g)] = gpool.tile([P, 512, 4], BF16, name="grouped_last", align_bytes=64)
-            nc.scalar.copy(out=grs[(su, g)][:], in_=pls[su][:, g * 4:(g + 1) * 4, :].rearrange("p j c -> p c j"))
+        def rg_v(su, g):
+            grs[(su, g)] = gpool.tile([P, 512, 4], BF16, name="grouped_v", align_bytes=64)
+            regroup(nc, False, grs[(su, g)][:], pls[su][:, g * 4:(g + 1) * 4, :])
+
+        def rg_halves(su, g):
+            gr = gpool.tile([P, 512, 4], BF16, name="grouped_last", align_bytes=64)
+            grs[(su, g)] = gr
+            src = pls[su][:, g * 4:(g + 1) * 4, :]
+            nc.scalar.copy(out=gr[:, 0:256, :], in_=src[:, :, 0:256].rearrange("p j c -> p c j"))
+            regroup(nc, True, gr[:, 256:512, :], src[:, :, 256:512])
+
+        def quant_half(su, g, tbl):
+            if g == 0 and tbl == 0:
+                cds[su] = qpool.tile([P, C * 512], U32, name="codes", align_bytes=64)
+                scs[su] = qpool.tile([P, C * 512], U8, name="scl", align_bytes=64)
+            o = g * 512 + tbl * 256
+            nc.vector.quantize_mx(
+                out=cds[su][:, o:o + 256].bitcast(FP8X4),
+                scales=scs[su][:, o:o + 256],
+                in_=grs[(su, g)][:, tbl * 256:(tbl + 1) * 256, :].rearrange("p c j -> p (c j)"),
+            )
 
         def rg(su, g):
             grs[(su, g)] = gpool.tile([P, 512, 4], BF16, name="grouped", align_bytes=64)
@@ -281,7 +308,10 @@ def tile_bandsplitmodule_t_kernel(tc, x_real, x_imag, ln_w, ln_b, fc_w, fc_b, ou
         def mx(su, tbl, e):
             n = (su // 2) % NB
             m = tbl * 2 + e
-            z = ps_z.tile([P, EMB], F32, name="z")
+            if su >= NSU - 2 and tbl == 1:
+                z = ps_x.tile([P, 512], F32, name="xt")
+            else:
+                z = ps_z.tile([P, EMB], F32, name="z")
             zss[(su, tbl, e)] = z
             for g in range(C):
                 lo = g * 512 + m * P
@@ -304,8 +334,10 @@ def tile_bandsplitmodule_t_kernel(tc, x_real, x_imag, ln_w, ln_b, fc_w, fc_b, ou
             zo = zos[(su, tbl)]
             nc.vector.tensor_tensor(out=zo[:, e, :], in0=zss[(su, tbl, e)][:], in1=bias_bf[:, n * EMB:(n + 1) * EMB],
                                     op=ALU.add)
-            if e == 1:
-                t0 = half * 512 + tbl * 256
+            t0 = half * 512 + tbl * 256
+            if su == NSU - 1:
+                nc.sync.dma_start(out=out[b, n, t0:t0 + 256, :].rearrange("(w e) d -> w e d", e=2)[:, e, :], in_=zo[:, e, :])
+            elif e == 1:
                 nc.sync.dma_start(out=out[b, n, t0:t0 + 256, :].rearrange("(w e) d -> w e d", e=2), in_=zo[:])
 
         for step in range(-2, NU - 1):
@@ -398,60 +430,55 @@ def tile_bandsplitmodule_t_kernel(tc, x_real, x_imag, ln_w, ln_b, fc_w, fc_b, ou
         u = NU - 1
         su = NSU - 1
         t2(su - 1, 1, 1)
+        t2(su - 1, 1, 2, spare=True)
+        t2(su - 1, 1, 3, spare=True)
         mx(su - 2, 0, 0)
         mx(su - 2, 0, 1)
-        p2(u, 0, 0)
         p3(su - 1, 1, 0)
-        t2(su - 1, 1, 2)
         p3v(su - 1, 1, 1)
-        p2(u, 0, 1)
-        t2(su - 1, 1, 3)
-        ev(su - 2, 0, 0)
-        ev(su - 2, 0, 1)
+        p2(u, 0, 0)
         p3(su - 1, 1, 2)
-        t2(su, 0, 0)
-        p2(u, 1, 0)
+        p2(u, 0, 1)
         p3v(su - 1, 1, 3)
-        t2(su, 0, 1)
-        p2(u, 1, 1)
-        t2(su, 0, 2, spare=True)
-        t2(su, 0, 3, spare=True)
+        p2(u, 1, 0)
+        ev(su - 2, 0, 0)
         quant(su - 1, 0)
         rg(su - 1, 1)
+        p2(u, 1, 1)
+        t2(su, 0, 0)
+        t2(su, 0, 1)
+        t2(su, 0, 2, spare=True)
+        t2(su, 0, 3, spare=True)
+        ev(su - 2, 0, 1)
         p3(su, 0, 0)
-        p3v(su, 0, 1)
+        p3(su, 0, 1)
+        mx(su - 2, 1, 0)
+        mx(su - 2, 1, 1)
         t2(su, 1, 0)
         t2(su, 1, 1)
         p3(su, 0, 2)
-        p3v(su, 0, 3)
+        p3(su, 0, 3)
         t2(su, 1, 2, spare=True)
         t2(su, 1, 3, spare=True)
-        p3(su, 1, 0)
-        p3v(su, 1, 1)
-        p3(su, 1, 2)
+        for e in range(2):
+            ev(su - 2, 1, e)
         quant(su - 1, 1)
+        rg_v(su, 0)
+        p3(su, 1, 0)
+        p3(su, 1, 1)
+        p3(su, 1, 2)
         p3(su, 1, 3)
-        rg(su, 0)
-        rg_last(su, 1)
-        mx(su - 2, 1, 0)
-        mx(su - 2, 1, 1)
-        ev(su - 2, 1, 0)
-        ev(su - 2, 1, 1)
-        mx(su - 1, 0, 0)
-        mx(su - 1, 0, 1)
-        ev(su - 1, 0, 0)
-        ev(su - 1, 0, 1)
-        quant(su, 0)
-        quant(su, 1)
-        mx(su - 1, 1, 0)
-        mx(su - 1, 1, 1)
-        ev(su - 1, 1, 0)
-        ev(su - 1, 1, 1)
-        mx(su, 0, 0)
-        mx(su, 0, 1)
-        ev(su, 0, 0)
-        ev(su, 0, 1)
-        mx(su, 1, 0)
-        mx(su, 1, 1)
-        ev(su, 1, 0)
-        ev(su, 1, 1)
+        rg_halves(su, 1)
+        for tbl in range(2):
+            for e in range(2):
+                mx(su - 1, tbl, e)
+            for e in range(2):
+                ev(su - 1, tbl, e)
+        for tbl in range(2):
+            for g in range(C):
+                quant_half(su, g, tbl)
+            for e in range(2):
+                mx(su, tbl, e)
+        for tbl in range(2):
+            for e in range(2):
+                ev(su, tbl, e)

@@ -20,8 +20,9 @@ FLOPS = 2 * B * NB * T * FEAT * EMB
 RG_ON_GPSIMD = True
 MANUAL = True
 XS_BUFS = 5
-GRAM = set(u for u in range(7, 32) if u % 2 or u % 8 == 4)
-VS = {u: (2,) if 6 <= u < 29 and u % 4 != 2 else () for u in range(0, 30)}
+DM = (0, 1, 1, 1)
+GRAM = set(u for u in range(7, 32) if u % 4 != 2)
+VS = {u: (2,) if 6 <= u < 29 and True else () for u in range(0, 30)}
 NU = B * NB * 4
 NSU = NU // 2
 
@@ -131,8 +132,9 @@ def tile_bandsplitmodule_t_kernel(tc, x_real, x_imag, ln_w, ln_b, fc_w, fc_b, ou
         ident = const.tile([P, P], F32)
         make_identity(nc, ident[:])
 
-        ones_bf = const.tile([P, 2], BF16)
-        nc.vector.memset(ones_bf[:], 1.0)
+        mean_bf = const.tile([P, 2], BF16)
+        nc.vector.memset(mean_bf[:, 0:1], 1.0 / FEAT)
+        nc.vector.memset(mean_bf[:, 1:2], -1.0 / FEAT)
         wsc = const.tile([P, NB * C * 4], F32)
         bsc = const.tile([P, NB * C * 4], F32)
 
@@ -162,7 +164,7 @@ def tile_bandsplitmodule_t_kernel(tc, x_real, x_imag, ln_w, ln_b, fc_w, fc_b, ou
             xt_in, span, t0 = x_units[u]
             xw = xt_in[:].bitcast(F32)
             xt = ps_x.tile([P, 512], F32, name="xt")
-            if u not in GRAM:
+            if u not in GRAM and (DM[k] or u < 6):
                 warm_pe(xt)
             for sl in range(4):
                 h, r = divmod(sl, 2)
@@ -199,25 +201,22 @@ def tile_bandsplitmodule_t_kernel(tc, x_real, x_imag, ln_w, ln_b, fc_w, fc_b, ou
                     if ph == 0:
                         nc.tensor.matmul(out=gb[:, 0:P], lhsT=xe, rhs=xe, start=(s == 0), stop=(s == 7))
                     else:
-                        nc.tensor.matmul(out=gb[:, P:P + 2], lhsT=xe, rhs=ones_bf[:], start=(s == 0), stop=(s == 7))
+                        nc.tensor.matmul(out=gb[:, P:P + 2], lhsT=xe, rhs=mean_bf[:], start=(s == 0), stop=(s == 7))
 
         def diag(u):
             gb = grams[u]
             mvs[u] = small.tile([P, 2, 2], F32, name="mv")
             mv = mvs[u]
             ex2 = small.tile([P, 1], F32, name="ex2")
-            mq = small.tile([P, 1], F32, name="mq")
             junk = small.tile([P, P], F32, name="junk")
             nc.vector.scalar_tensor_tensor(out=junk[:], in0=gb[:, 0:P], scalar=1.0 / FEAT, in1=ident[:], op0=ALU.mult,
                                            op1=ALU.mult, accum_out=ex2[:])
-            nc.vector.tensor_scalar(out=mq[:], in0=gb[:, P:P + 1], scalar1=-1.0 / FEAT / FEAT, scalar2=None, op0=ALU.mult)
-            nc.vector.tensor_scalar(out=mv[:, 1, 0:1], in0=gb[:, P:P + 1], scalar1=1.0 / FEAT, scalar2=None, op0=ALU.mult)
-            ex2s[u] = (ex2, mq)
+            nc.vector.tensor_copy(out=mv[:, 1, 0:1], in_=gb[:, P:P + 1])
+            ex2s[u] = ex2
 
         def diag2(u):
-            ex2, mq = ex2s[u]
-            nc.vector.scalar_tensor_tensor(out=mvs[u][:, 1, 1:2], in0=grams[u][:, P:P + 1], scalar=mq[:], in1=ex2[:],
-                                           op0=ALU.mult, op1=ALU.add)
+            nc.vector.scalar_tensor_tensor(out=mvs[u][:, 1, 1:2], in0=grams[u][:, P:P + 1], scalar=grams[u][:, P + 1:P + 2],
+                                           in1=ex2s[u][:], op0=ALU.mult, op1=ALU.add)
 
 
         def rcp(u):
@@ -241,7 +240,7 @@ def tile_bandsplitmodule_t_kernel(tc, x_real, x_imag, ln_w, ln_b, fc_w, fc_b, ou
                 vt = ps_v.tile([P, 512], F32, name="vt")
             vts[(su, s)] = vt
             uu = 2 * su + g + 4 if j else 2 * su + g + 3
-            if j in (0, 3) and uu not in GRAM:
+            if (j == 0 and (DM[3] or uu < 6) or j == 3 and (DM[2] or uu < 6)) and uu not in GRAM:
                 warm_pe(vt)
             for m in range(4):
                 tbl, e = divmod(m, 2)

@@ -20,8 +20,7 @@ FLOPS = 2 * B * NB * T * FEAT * EMB
 RG_ON_GPSIMD = True
 MANUAL = True
 XS_BUFS = 5
-DM = (0, 1, 1, 1)
-GRAM = set(u for u in range(7, 32) if u % 4 != 2)
+FIRST_GRAM = 7
 VS = {u: (2,) if 6 <= u < 29 and True else () for u in range(0, 30)}
 NU = B * NB * 4
 NSU = NU // 2
@@ -156,16 +155,11 @@ def tile_bandsplitmodule_t_kernel(tc, x_real, x_imag, ln_w, ln_b, fc_w, fc_b, ou
         zss = {}
         zos = {}
 
-        def warm_pe(bank):
-            nc.tensor.matmul(out=bank[:, 0:P], lhsT=ident[:], rhs=ident[:], start=True, stop=True)
-
         def t1k(u, k):
             i, q = divmod(u, 4)
             xt_in, span, t0 = x_units[u]
             xw = xt_in[:].bitcast(F32)
             xt = ps_x.tile([P, 512], F32, name="xt")
-            if u not in GRAM and (DM[k] or u < 6):
-                warm_pe(xt)
             for sl in range(4):
                 h, r = divmod(sl, 2)
                 o = (((k * 2 + r) * 2 + h) * span + t0) // 2
@@ -180,10 +174,10 @@ def tile_bandsplitmodule_t_kernel(tc, x_real, x_imag, ln_w, ln_b, fc_w, fc_b, ou
             nc.vector.bn_stats(out=sts[u][:, e, k, :], in_=banks[(u, k)][:, :, e])
 
         def aggr(u):
-            if u not in GRAM:
+            if u < FIRST_GRAM:
                 mvs[u] = small.tile([P, 2, 2], F32, name="mv")
             mv = mvs[u]
-            for e in range(1 if u in GRAM else 2):
+            for e in range(1 if u >= FIRST_GRAM else 2):
                 nc.vector.bn_aggr(out=mv[:, e, :], in_=sts[u][:, e].rearrange("p k s -> p (k s)"))
 
         def sqrt_(u):
@@ -239,9 +233,6 @@ def tile_bandsplitmodule_t_kernel(tc, x_real, x_imag, ln_w, ln_b, fc_w, fc_b, ou
             else:
                 vt = ps_v.tile([P, 512], F32, name="vt")
             vts[(su, s)] = vt
-            uu = 2 * su + g + 4 if j else 2 * su + g + 3
-            if (j == 0 and (DM[3] or uu < 6) or j == 3 and (DM[2] or uu < 6)) and uu not in GRAM:
-                warm_pe(vt)
             for m in range(4):
                 tbl, e = divmod(m, 2)
                 nc.tensor.transpose(out=vt[:, m * P:(m + 1) * P], in_=vs[su][:, tbl, e, s * P:(s + 1) * P],
@@ -351,7 +342,7 @@ def tile_bandsplitmodule_t_kernel(tc, x_real, x_imag, ln_w, ln_b, fc_w, fc_b, ou
             do_st = 0 <= step + 1 < NU
             do_t1 = 0 <= step + 2 < NU
 
-            gu = do_st and step + 1 in GRAM
+            gu = do_st and step + 1 >= FIRST_GRAM
             if gu:
                 diag(step + 1)
             if do_st:
@@ -387,7 +378,7 @@ def tile_bandsplitmodule_t_kernel(tc, x_real, x_imag, ln_w, ln_b, fc_w, fc_b, ou
                 aggr(step + 1)
             if do_mx:
                 ev(km, tblm, 1)
-            if do_t1 and step + 2 in GRAM:
+            if do_t1 and step + 2 >= FIRST_GRAM:
                 gram(step + 2)
             if do_p2:
                 p2(step, 1, 0)

@@ -21,7 +21,7 @@ RG_ON_GPSIMD = True
 MANUAL = True
 XS_BUFS = 5
 FIRST_GRAM = 7
-VS = {u: (2,) if 6 <= u < 29 and True else () for u in range(0, 30)}
+VS = {u: (2,) if u < 29 else () for u in range(0, 30)}
 NU = B * NB * 4
 NSU = NU // 2
 
@@ -196,6 +196,19 @@ def tile_bandsplitmodule_t_kernel(tc, x_real, x_imag, ln_w, ln_b, fc_w, fc_b, ou
                         nc.tensor.matmul(out=gb[:, 0:P], lhsT=xe, rhs=xe, start=(s == 0), stop=(s == 7))
                     else:
                         nc.tensor.matmul(out=gb[:, P:P + 2], lhsT=xe, rhs=mean_bf[:], start=(s == 0), stop=(s == 7))
+
+        def keep_clock(su, n):
+            idle = ps_z.tile([P, EMB], F32, name="z")
+            for i in range(n):
+                nc.tensor.matmul_mx(
+                    out=idle[:],
+                    lhsT=cds[su][:, 0:P].bitcast(FP8X4),
+                    lhsT_scale=scs[su][:, 0:P],
+                    rhs=wcodes[:, 0:EMB].bitcast(FP8X4),
+                    rhs_scale=wscales[:, 0:EMB],
+                    start=True,
+                    stop=True,
+                )
 
         def diag(u):
             gb = grams[u]
@@ -380,6 +393,8 @@ def tile_bandsplitmodule_t_kernel(tc, x_real, x_imag, ln_w, ln_b, fc_w, fc_b, ou
                 ev(km, tblm, 1)
             if do_t1 and step + 2 >= FIRST_GRAM:
                 gram(step + 2)
+            if not do_t1:
+                keep_clock(km, 2)
             if do_p2:
                 p2(step, 1, 0)
             if do_st:
@@ -394,12 +409,12 @@ def tile_bandsplitmodule_t_kernel(tc, x_real, x_imag, ln_w, ln_b, fc_w, fc_b, ou
                 t1k(step + 2, 1)
             if do_p3:
                 p3(kp, g, 3)
-            if do_st:
+            if do_st and step >= 5:
                 rcp(step + 1)
             if step == 0:
                 for n in range(NB):
-                    nc.vector.tensor_copy(out=wsc[:, n * 8:(n + 1) * 8], in_=wls[n][:].rearrange("p c j -> p (c j)"))
-                    nc.vector.tensor_copy(out=bsc[:, n * 8:(n + 1) * 8], in_=bls[n][:].rearrange("p c j -> p (c j)"))
+                    nc.scalar.copy(out=wsc[:, n * 8:(n + 1) * 8], in_=wls[n][:].rearrange("p c j -> p (c j)"))
+                    nc.scalar.copy(out=bsc[:, n * 8:(n + 1) * 8], in_=bls[n][:].rearrange("p c j -> p (c j)"))
             if step in (0, 0 + 1):
                 gate = const.tile([P, 1], F32, name="gate%d" % (step - (0)))
                 nc.vector.memset(gate[:], 1.0)
@@ -414,6 +429,8 @@ def tile_bandsplitmodule_t_kernel(tc, x_real, x_imag, ln_w, ln_b, fc_w, fc_b, ou
                 quant_w(1)
             if 0 <= kq < NSU:
                 quant(kq, gq)
+            if do_st and step < 5:
+                rcp(step + 1)
             if do_p3:
                 rg(kp, g)
 
@@ -464,6 +481,7 @@ def tile_bandsplitmodule_t_kernel(tc, x_real, x_imag, ln_w, ln_b, fc_w, fc_b, ou
                 mx(su - 1, tbl, e)
             for e in range(2):
                 ev(su - 1, tbl, e)
+        keep_clock(su - 1, 3)
         for tbl in range(2):
             for g in range(C):
                 quant_half(su, g, tbl)

@@ -21,7 +21,7 @@ RG_ON_GPSIMD = True
 MANUAL = True
 XS_BUFS = 5
 FIRST_GRAM = 7
-VS = {u: (2,) if u < 29 else () for u in range(0, 30)}
+VS = {u: ((2, 3) if u >= 8 and u % 8 == 4 else (2,)) if u < 29 else () for u in range(0, 30)}
 NU = B * NB * 4
 NSU = NU // 2
 
@@ -415,16 +415,16 @@ def tile_bandsplitmodule_t_kernel(tc, x_real, x_imag, ln_w, ln_b, fc_w, fc_b, ou
                 for n in range(NB):
                     nc.scalar.copy(out=wsc[:, n * 8:(n + 1) * 8], in_=wls[n][:].rearrange("p c j -> p (c j)"))
                     nc.scalar.copy(out=bsc[:, n * 8:(n + 1) * 8], in_=bls[n][:].rearrange("p c j -> p (c j)"))
-            if step in (0, 0 + 1):
-                gate = const.tile([P, 1], F32, name="gate%d" % (step - (0)))
+            if step in (0, 1):
+                gate = const.tile([P, 1], F32, name="gate%d" % step)
                 nc.vector.memset(gate[:], 1.0)
-                regroup(nc, True, wgrps[0][:, step - (0)], wraws[0][:, step - (0)], one=gate[:, 0:1])
+                regroup(nc, True, wgrps[0][:, step], wraws[0][:, step], one=gate[:, 0:1])
             if step == 2:
                 quant_w(0)
             if 3 <= step < 3 + 4:
                 q = step - 3
                 lo = (q % 2) * 256
-                regroup(nc, True, wgrps[1][:, q // 2, lo:lo + 256], wraws[1][:, q // 2, :, lo:lo + 256])
+                regroup(nc, False, wgrps[1][:, q // 2, lo:lo + 256], wraws[1][:, q // 2, :, lo:lo + 256])
             if step == 7:
                 quant_w(1)
             if 0 <= kq < NSU:

from contextlib import ExitStack

import concourse.mybir as mybir
from concourse.masks import make_identity

F32 = mybir.dt.float32
BF16 = mybir.dt.bfloat16
U32 = mybir.dt.uint32
U8 = mybir.dt.uint8
FP8X4 = mybir.dt.float8_e4m3fn_x4
ALU = mybir.AluOpType
ACTF = mybir.ActivationFunctionType

B, C, NB, BW, T, EMB = 4, 2, 2, 256, 1024, 512
FEAT = C * BW * 2
EPS = 1e-5
P = 128
FLOPS = 2 * B * NB * T * FEAT * EMB

RG_ON_GPSIMD = True
MANUAL = True
XS_BUFS = 5
FIRST_GRAM = 7
VS = {u: ((2, 3) if u >= 8 and u % 8 == 4 else (2,)) if u < 29 else () for u in range(0, 30)}
NU = B * NB * 4
NSU = NU // 2


def regroup(nc, on_gpsimd, dst, src, one=1.0):
    if on_gpsimd:
        nc.gpsimd.tensor_scalar(
            out=dst, in0=src.rearrange("p j c -> p c j"), scalar1=one, scalar2=0.0,
            op0=ALU.mult, op1=ALU.add,
        )
    else:
        nc.vector.tensor_copy(
            out=dst.rearrange("p (c i) j -> p c j i", i=4),
            in_=src.rearrange("p j (c i) -> p c j i", i=4),
        )


def tile_bandsplitmodule_t_kernel(tc, x_real, x_imag, ln_w, ln_b, fc_w, fc_b, out):
    nc = tc.nc
    with ExitStack() as ctx:
        const = ctx.enter_context(tc.tile_pool(name="const", bufs=1))
        wstage = ctx.enter_context(tc.tile_pool(name="wstage", bufs=1))
        xpool = ctx.enter_context(tc.tile_pool(name="xpool", bufs=XS_BUFS))
        small = ctx.enter_context(tc.tile_pool(name="small", bufs=4))
        vpool = ctx.enter_context(tc.tile_pool(name="vpool", bufs=2))
        ppool = ctx.enter_context(tc.tile_pool(name="ppool", bufs=2))
        gpool = ctx.enter_context(tc.tile_pool(name="gpool", bufs=1))
        qpool = ctx.enter_context(tc.tile_pool(name="qpool", bufs=2))
        opool = ctx.enter_context(tc.tile_pool(name="opool", bufs=4))
        ps_x = ctx.enter_context(tc.psum_pool(name="ps_x", bufs=4))
        ps_v = ctx.enter_context(tc.psum_pool(name="ps_v", bufs=2))
        ps_z = ctx.enter_context(tc.psum_pool(name="ps_z", bufs=2))
        if MANUAL:
            ctx.enter_context(tc.manual_schedule())

        x_units = {}
        wgrps = {}
        wraws = {}
        banks = {}
        sts = {}
        mvs = {}
        sds = {}
        rss = {}
        nms = {}
        vs = {}
        pls = {}
        grs = {}
        cds = {}
        scs = {}
        vts = {}
        grams = {}
        ex2s = {}

        def load_part(dst, b, n, c, r, t0, w):
            src = (x_real if r == 0 else x_imag)[b, c, n * BW:(n + 1) * BW, t0:t0 + w]
            nc.sync.dma_start(out=dst.rearrange("p (h t) -> p h t", h=2), in_=src.rearrange("(p h) t -> p h t", h=2))

        def load_x(i):
            b, n = divmod(i, NB)
            xs = xpool.tile([P, 8 * T], BF16, name="xs")
            for q in range(4):
                x_units[i * 4 + q] = (xs, T, q * 256)
            for c in range(C):
                for r in range(2):
                    o = (c * 2 + r) * 2 * T
                    load_part(xs[:, o:o + 2 * T], b, n, c, r, 0, T)

        def load_x0(q):
            xq = wstage.tile([P, 8 * 256], BF16, name="xq%d" % q)
            x_units[q] = (xq, 256, 0)
            for c in range(C):
                for r in range(2):
                    o = (c * 2 + r) * 2 * 256
                    load_part(xq[:, o:o + 512], 0, 0, c, r, q * 256, 256)

        def load_w(n):
            wraw = wstage.tile([P, C, 4, EMB], BF16, name="wraw%d" % n)
            nc.sync.dma_start(out=wraw[:].rearrange("p g j e -> p g (j e)"),
                              in_=fc_w[n].rearrange("(g p j) e -> p g (j e)", g=C, j=4))
            return wraw

        load_x0(0)
        load_x0(1)
        wls = {}
        bls = {}
        for n in range(NB):
            wls[n] = const.tile([P, C, 4], BF16, name="wl%d" % n)
            bls[n] = const.tile([P, C, 4], BF16, name="bl%d" % n)
            nc.sync.dma_start(out=wls[n][:], in_=ln_w[n].rearrange("(c p j) -> p c j", c=C, j=4))
            nc.sync.dma_start(out=bls[n][:], in_=ln_b[n].rearrange("(c p j) -> p c j", c=C, j=4))
        load_x0(2)
        load_x0(3)
        wraw0 = load_w(0)
        load_x(1)
        bias_bf = const.tile([P, NB * EMB], BF16)
        nc.sync.dma_start(out=bias_bf[:], in_=fc_b.rearrange("n e -> (n e)").partition_broadcast(P))
        wraw1 = load_w(1)
        for i in range(2, 1 + XS_BUFS):
            load_x(i)

        zero_t = const.tile([P, 1], F32)
        nc.vector.memset(zero_t[:], 0.0)
        eps_t = const.tile([P, 1], F32)
        nc.vector.tensor_scalar(out=eps_t[:], in0=zero_t[:], scalar1=EPS, scalar2=None, op0=ALU.add)
        warm = const.tile([P, 1], F32)
        nc.scalar.activation(out=warm[:], in_=eps_t[:], func=ACTF.Abs_reciprocal_sqrt)
        ident = const.tile([P, P], F32)
        make_identity(nc, ident[:])

        mean_bf = const.tile([P, 2], BF16)
        nc.vector.memset(mean_bf[:, 0:1], 1.0 / FEAT)
        nc.vector.memset(mean_bf[:, 1:2], -1.0 / FEAT)
        wsc = const.tile([P, NB * C * 4], F32)
        bsc = const.tile([P, NB * C * 4], F32)

        wcodes = const.tile([P, NB * C * EMB], U32, align_bytes=64)
        wscales = const.tile([P, NB * C * EMB], U8, align_bytes=64)
        for n, wraw in ((0, wraw0), (1, wraw1)):
            wgrp = wstage.tile([P, C, EMB, 4], BF16, name="wgrp%d" % n, align_bytes=64)
            wgrps[n] = wgrp
            wraws[n] = wraw

        def quant_w(n):
            o = n * C * EMB
            nc.vector.quantize_mx(
                out=wcodes[:, o:o + C * EMB].bitcast(FP8X4),
                scales=wscales[:, o:o + C * EMB],
                in_=wgrps[n][:].rearrange("p g e j -> p (g e j)"),
            )

        zss = {}
        zos = {}

        def t1k(u, k):
            i, q = divmod(u, 4)
            xt_in, span, t0 = x_units[u]
            xw = xt_in[:].bitcast(F32)
            xt = ps_x.tile([P, 512], F32, name="xt")
            for sl in range(4):
                h, r = divmod(sl, 2)
                o = (((k * 2 + r) * 2 + h) * span + t0) // 2
                nc.tensor.transpose(out=xt[:, sl * P:(sl + 1) * P], in_=xw[:, o:o + P], identity=ident[:])
            banks[(u, k)] = xt[:].bitcast(BF16).rearrange("w (q e) -> w q e", e=2)
            if k == 1 and q == 3 and i > 0 and i + XS_BUFS < B * NB:
                load_x(i + XS_BUFS)

        def bn(u, k, e):
            if k == 0 and e == 0:
                sts[u] = small.tile([P, 2, 2, 6], F32, name="st")
            nc.vector.bn_stats(out=sts[u][:, e, k, :], in_=banks[(u, k)][:, :, e])

        def aggr(u):
            if u < FIRST_GRAM:
                mvs[u] = small.tile([P, 2, 2], F32, name="mv")
            mv = mvs[u]
            for e in range(1 if u >= FIRST_GRAM else 2):
                nc.vector.bn_aggr(out=mv[:, e, :], in_=sts[u][:, e].rearrange("p k s -> p (k s)"))

        def sqrt_(u):
            rs = small.tile([P, 2], F32, name="rs")
            rss[u] = rs
            nc.scalar.activation(out=rs[:], in_=mvs[u][:, :, 1], func=ACTF.Abs_reciprocal_sqrt, bias=eps_t[:], scale=1.0)

        def gram(u):
            xs, span, t0 = x_units[u]
            gb = ps_z.tile([P, EMB], F32, name="z")
            grams[u] = gb
            for ph in range(2):
                for s in range(8):
                    xe = xs[:, s * span + t0 + 1:s * span + t0 + 256:2]
                    if ph == 0:
                        nc.tensor.matmul(out=gb[:, 0:P], lhsT=xe, rhs=xe, start=(s == 0), stop=(s == 7))
                    else:
                        nc.tensor.matmul(out=gb[:, P:P + 2], lhsT=xe, rhs=mean_bf[:], start=(s == 0), stop=(s == 7))

        def keep_clock(su, n):
            idle = ps_z.tile([P, EMB], F32, name="z")
            for i in range(n):
                nc.tensor.matmul_mx(
                    out=idle[:],
                    lhsT=cds[su][:, 0:P].bitcast(FP8X4),
                    lhsT_scale=scs[su][:, 0:P],
                    rhs=wcodes[:, 0:EMB].bitcast(FP8X4),
                    rhs_scale=wscales[:, 0:EMB],
                    start=True,
                    stop=True,
                )

        def diag(u):
            gb = grams[u]
            mvs[u] = small.tile([P, 2, 2], F32, name="mv")
            mv = mvs[u]
            ex2 = small.tile([P, 1], F32, name="ex2")
            junk = small.tile([P, P], F32, name="junk")
            nc.vector.scalar_tensor_tensor(out=junk[:], in0=gb[:, 0:P], scalar=1.0 / FEAT, in1=ident[:], op0=ALU.mult,
                                           op1=ALU.mult, accum_out=ex2[:])
            nc.vector.tensor_copy(out=mv[:, 1, 0:1], in_=gb[:, P:P + 1])
            ex2s[u] = ex2

        def diag2(u):
            nc.vector.scalar_tensor_tensor(out=mvs[u][:, 1, 1:2], in0=grams[u][:, P:P + 1], scalar=grams[u][:, P + 1:P + 2],
                                           in1=ex2s[u][:], op0=ALU.mult, op1=ALU.add)


        def rcp(u):
            nm = small.tile([P, 2], F32, name="nm")
            nms[u] = nm
            nc.vector.scalar_tensor_tensor(out=nm[:], in0=mvs[u][:, :, 0], scalar=-1.0, in1=rss[u][:],
                                           op0=ALU.mult, op1=ALU.mult)

        def p2(u, k, e):
            su, tbl = divmod(u, 2)
            if tbl == 0 and k == 0 and e == 0:
                vs[su] = vpool.tile([P, 2, 2, FEAT], F32, name="v")
            nc.scalar.activation(out=vs[su][:, tbl, e, k * 512:(k + 1) * 512], in_=banks[(u, k)][:, :, e],
                                 func=ACTF.Identity, scale=rss[u][:, e:e + 1], bias=nms[u][:, e:e + 1])

        def t2(su, g, j, spare=False):
            s = g * 4 + j
            if spare:
                vt = ps_x.tile([P, 512], F32, name="xt")
            else:
                vt = ps_v.tile([P, 512], F32, name="vt")
            vts[(su, s)] = vt
            for m in range(4):
                tbl, e = divmod(m, 2)
                nc.tensor.transpose(out=vt[:, m * P:(m + 1) * P], in_=vs[su][:, tbl, e, s * P:(s + 1) * P],
                                    identity=ident[:])

        def p3(su, g, j):
            s = g * 4 + j
            n = (su // 2) % NB
            if s == 0:
                pls[su] = ppool.tile([P, 8, 512], BF16, name="planes")
            col = n * 8 + s
            if j in VS.get(su * 2 + g, ()):
                nc.vector.tensor_scalar(out=pls[su][:, s, :], in0=vts[(su, s)][:], scalar1=wsc[:, col:col + 1],
                                        scalar2=bsc[:, col:col + 1], op0=ALU.mult, op1=ALU.add)
            else:
                nc.scalar.activation(out=pls[su][:, s, :], in_=vts[(su, s)][:], func=ACTF.Identity,
                                     scale=wsc[:, col:col + 1], bias=bsc[:, col:col + 1])

        def p3v(su, g, j):
            s = g * 4 + j
            if s == 0:
                pls[su] = ppool.tile([P, 8, 512], BF16, name="planes")
            col = ((su // 2) % NB) * 8 + s
            nc.vector.tensor_scalar(out=pls[su][:, s, :], in0=vts[(su, s)][:], scalar1=wsc[:, col:col + 1],
                                    scalar2=bsc[:, col:col + 1], op0=ALU.mult, op1=ALU.add)

        def rg_v(su, g):
            grs[(su, g)] = gpool.tile([P, 512, 4], BF16, name="grouped_v", align_bytes=64)
            regroup(nc, False, grs[(su, g)][:], pls[su][:, g * 4:(g + 1) * 4, :])

        def rg_halves(su, g):
            gr = gpool.tile([P, 512, 4], BF16, name="grouped_last", align_bytes=64)
            grs[(su, g)] = gr
            src = pls[su][:, g * 4:(g + 1) * 4, :]
            nc.scalar.copy(out=gr[:, 0:256, :], in_=src[:, :, 0:256].rearrange("p j c -> p c j"))
            regroup(nc, True, gr[:, 256:512, :], src[:, :, 256:512])

        def quant_half(su, g, tbl):
            if g == 0 and tbl == 0:
                cds[su] = qpool.tile([P, C * 512], U32, name="codes", align_bytes=64)
                scs[su] = qpool.tile([P, C * 512], U8, name="scl", align_bytes=64)
            o = g * 512 + tbl * 256
            nc.vector.quantize_mx(
                out=cds[su][:, o:o + 256].bitcast(FP8X4),
                scales=scs[su][:, o:o + 256],
                in_=grs[(su, g)][:, tbl * 256:(tbl + 1) * 256, :].rearrange("p c j -> p (c j)"),
            )

        def rg(su, g):
            grs[(su, g)] = gpool.tile([P, 512, 4], BF16, name="grouped", align_bytes=64)
            regroup(nc, RG_ON_GPSIMD, grs[(su, g)][:], pls[su][:, g * 4:(g + 1) * 4, :])

        def quant(su, g):
            if g == 0:
                cds[su] = qpool.tile([P, C * 512], U32, name="codes", align_bytes=64)
                scs[su] = qpool.tile([P, C * 512], U8, name="scl", align_bytes=64)
            nc.vector.quantize_mx(
                out=cds[su][:, g * 512:(g + 1) * 512].bitcast(FP8X4),
                scales=scs[su][:, g * 512:(g + 1) * 512],
                in_=grs[(su, g)][:].rearrange("p c j -> p (c j)"),
            )

        def mx(su, tbl, e):
            n = (su // 2) % NB
            m = tbl * 2 + e
            if su >= NSU - 2 and tbl == 1:
                z = ps_x.tile([P, 512], F32, name="xt")
            else:
                z = ps_z.tile([P, EMB], F32, name="z")
            zss[(su, tbl, e)] = z
            for g in range(C):
                lo = g * 512 + m * P
                ro = (n * C + g) * EMB
                nc.tensor.matmul_mx(
                    out=z[:],
                    lhsT=cds[su][:, lo:lo + P].bitcast(FP8X4),
                    lhsT_scale=scs[su][:, lo:lo + P],
                    rhs=wcodes[:, ro:ro + EMB].bitcast(FP8X4),
                    rhs_scale=wscales[:, ro:ro + EMB],
                    start=(g == 0),
                    stop=(g == C - 1),
                )

        def ev(su, tbl, e):
            i, half = divmod(su, 2)
            b, n = divmod(i, NB)
            if e == 0:
                zos[(su, tbl)] = opool.tile([P, 2, EMB], F32, name="zo")
            zo = zos[(su, tbl)]
            nc.vector.tensor_tensor(out=zo[:, e, :], in0=zss[(su, tbl, e)][:], in1=bias_bf[:, n * EMB:(n + 1) * EMB],
                                    op=ALU.add)
            t0 = half * 512 + tbl * 256
            if su == NSU - 1:
                nc.sync.dma_start(out=out[b, n, t0:t0 + 256, :].rearrange("(w e) d -> w e d", e=2)[:, e, :], in_=zo[:, e, :])
            elif e == 1:
                nc.sync.dma_start(out=out[b, n, t0:t0 + 256, :].rearrange("(w e) d -> w e d", e=2), in_=zo[:])

        for step in range(-2, NU - 1):
            kp, g = divmod(step - 2, 2)
            do_p3 = 0 <= kp < NSU
            kn, gn = divmod(step - 1, 2)
            do_next = 0 <= kn < NSU
            kq, gq = divmod(step - 3, 2)
            km, tblm = divmod(step - 5, 2)
            do_mx = 0 <= km < NSU
            do_p2 = 0 <= step < NU
            do_st = 0 <= step + 1 < NU
            do_t1 = 0 <= step + 2 < NU

            gu = do_st and step + 1 >= FIRST_GRAM
            if gu:
                diag(step + 1)
            if do_st:
                bn(step + 1, 0, 0)
            if gu:
                diag2(step + 1)
            elif do_st:
                bn(step + 1, 0, 1)
            if do_st:
                bn(step + 1, 1, 0)
            if do_st and not gu:
                bn(step + 1, 1, 1)
            if do_p3:
                t2(kp, g, 1)
            if do_mx:
                mx(km, tblm, 0)
                mx(km, tblm, 1)
            if do_p2:
                p2(step, 0, 0)
            if do_p3:
                p3(kp, g, 0)
                t2(kp, g, 2)
            if do_p2:
                p2(step, 0, 1)
            if do_t1:
                t1k(step + 2, 0)
            if do_p3:
                p3(kp, g, 1)
                t2(kp, g, 3)
            if do_mx:
                ev(km, tblm, 0)
            if do_st:
                aggr(step + 1)
            if do_mx:
                ev(km, tblm, 1)
            if do_t1 and step + 2 >= FIRST_GRAM:
                gram(step + 2)
            if not do_t1:
                keep_clock(km, 2)
            if do_p2:
                p2(step, 1, 0)
            if do_st:
                sqrt_(step + 1)
            if do_p3:
                p3(kp, g, 2)
            if do_next:
                t2(kn, gn, 0)
            if do_p2:
                p2(step, 1, 1)
            if do_t1:
                t1k(step + 2, 1)
            if do_p3:
                p3(kp, g, 3)
            if do_st and step >= 5:
                rcp(step + 1)
            if step == 0:
                for n in range(NB):
                    nc.scalar.copy(out=wsc[:, n * 8:(n + 1) * 8], in_=wls[n][:].rearrange("p c j -> p (c j)"))
                    nc.scalar.copy(out=bsc[:, n * 8:(n + 1) * 8], in_=bls[n][:].rearrange("p c j -> p (c j)"))
            if step in (0, 1):
                gate = const.tile([P, 1], F32, name="gate%d" % step)
                nc.vector.memset(gate[:], 1.0)
                regroup(nc, True, wgrps[0][:, step], wraws[0][:, step], one=gate[:, 0:1])
            if step == 2:
                quant_w(0)
            if 3 <= step < 3 + 4:
                q = step - 3
                lo = (q % 2) * 256
                regroup(nc, False, wgrps[1][:, q // 2, lo:lo + 256], wraws[1][:, q // 2, :, lo:lo + 256])
            if step == 7:
                quant_w(1)
            if 0 <= kq < NSU:
                quant(kq, gq)
            if do_st and step < 5:
                rcp(step + 1)
            if do_p3:
                rg(kp, g)

        u = NU - 1
        su = NSU - 1
        t2(su - 1, 1, 1)
        t2(su - 1, 1, 2, spare=True)
        t2(su - 1, 1, 3, spare=True)
        mx(su - 2, 0, 0)
        mx(su - 2, 0, 1)
        p3(su - 1, 1, 0)
        p3v(su - 1, 1, 1)
        p2(u, 0, 0)
        p3(su - 1, 1, 2)
        p2(u, 0, 1)
        p3v(su - 1, 1, 3)
        p2(u, 1, 0)
        ev(su - 2, 0, 0)
        quant(su - 1, 0)
        rg(su - 1, 1)
        p2(u, 1, 1)
        t2(su, 0, 0)
        t2(su, 0, 1)
        t2(su, 0, 2, spare=True)
        t2(su, 0, 3, spare=True)
        ev(su - 2, 0, 1)
        p3(su, 0, 0)
        p3(su, 0, 1)
        mx(su - 2, 1, 0)
        mx(su - 2, 1, 1)
        t2(su, 1, 0)
        t2(su, 1, 1)
        p3(su, 0, 2)
        p3(su, 0, 3)
        t2(su, 1, 2, spare=True)
        t2(su, 1, 3, spare=True)
        for e in range(2):
            ev(su - 2, 1, e)
        quant(su - 1, 1)
        rg_v(su, 0)
        p3(su, 1, 0)
        p3(su, 1, 1)
        p3(su, 1, 2)
        p3(su, 1, 3)
        rg_halves(su, 1)
        for tbl in range(2):
            for e in range(2):
                mx(su - 1, tbl, e)
            for e in range(2):
                ev(su - 1, tbl, e)
        keep_clock(su - 1, 3)
        for tbl in range(2):
            for g in range(C):
                quant_half(su, g, tbl)
            for e in range(2):
                mx(su, tbl, e)
        for tbl in range(2):
            for e in range(2):
                ev(su, tbl, e)
